import numpy as np
import ml_dtypes


def mxq(x, axis, fmt="e4m3"):
    dtype, down = {"e4m3": (ml_dtypes.float8_e4m3fn, 7), "e5m2": (ml_dtypes.float8_e5m2, 14)}[fmt]
    v = np.moveaxis(np.asarray(x, np.float32).astype(ml_dtypes.bfloat16).astype(np.float64), axis, -1)
    blocks = v.reshape(v.shape[:-1] + (-1, 32))
    amax = np.abs(blocks).max(-1, keepdims=True)
    byte = np.maximum(np.where(amax > 0, np.frexp(amax)[1] - 1 + 127, 0) - down, 1)
    scale = np.exp2(byte - 127.0)
    codes = (blocks / scale).astype(np.float32).astype(dtype).astype(np.float64)
    return np.moveaxis((codes * scale).reshape(v.shape), -1, axis)


WIDE = False


def mx_kscale(k):
    if not WIDE:
        return np.ones(k)
    levels = np.array([10, -10, 5, -5, 0])
    if k % 512:
        return np.exp2(np.random.permutation(np.resize(levels, k // 32))).repeat(32)
    a = np.empty((k // 512, 16))
    for p in range(k // 512):
        a[p, :8] = np.random.permutation(np.resize(levels, 8))
        for g in range(8):
            far = levels[np.abs(levels - a[p, g]) >= 10]
            a[p, g + 8] = far[np.random.randint(len(far))]
    return np.exp2(a.ravel()).repeat(32)


BF16 = ml_dtypes.bfloat16


def bf(x):
    return np.asarray(x, np.float32).astype(BF16)


def f64(x):
    return np.asarray(x).astype(np.float64)


E2M1 = np.array([0.0, 0.5, 1.0, 1.5, 2.0, 3.0, 4.0, 6.0, -0.0, -0.5, -1.0, -1.5, -2.0, -3.0, -4.0, -6.0])


def pack_weight(w, fmt):
    k, n = w.shape
    w = f64(bf(w)).reshape(k // 32, 32, n)
    amax = np.abs(w).max(1)
    if fmt == "e4m3":
        byte = np.frexp(amax)[1] - 1 + 127 - 7
    else:
        mant, ex = np.frexp(amax / 6.0)
        byte = np.where(mant > 0.5, ex, ex - 1) + 127
    byte = np.clip(np.where(amax > 0, byte, 1), 1, 254)
    scaled = (w * np.exp2(127.0 - byte)[:, None, :]).reshape(k, n).astype(np.float32)
    by_word = np.ascontiguousarray(scaled.reshape(k // 512, 128, 4, n).transpose(0, 1, 3, 2))
    if fmt == "e4m3":
        words = by_word.astype(ml_dtypes.float8_e4m3fn).view(np.uint8)
    else:
        c = by_word.astype(ml_dtypes.float4_e2m1fn).view(np.uint8) & 0xF
        words = c[..., 0::2] | (c[..., 1::2] << 4)
    return np.ascontiguousarray(words), np.ascontiguousarray(byte.astype(np.uint8).reshape(k // 512, 16, n))


def unpack_weight(words, scales, fmt):
    g, p, n, _ = words.shape
    if fmt == "e4m3":
        vals = np.ascontiguousarray(words).view(ml_dtypes.float8_e4m3fn).astype(np.float64)
    else:
        nib = np.empty((g, p, n, 4), np.uint8)
        nib[..., 0::2] = words & 0xF
        nib[..., 1::2] = words >> 4
        vals = E2M1[nib]
    vals = vals * np.repeat(np.exp2(scales.astype(np.float64) - 127.0), 8, axis=1)[..., None]
    return vals.transpose(0, 1, 3, 2).reshape(g * 512, n)
def pack4(w):
    words, scales = pack_weight(w, "e2m1")
    return words.reshape(words.shape[0], 128, -1), scales


def unpack4(words, scales):
    return unpack_weight(words.reshape(words.shape[0], 128, -1, 2), scales, "e2m1")


B, N, VF_D, HID_D, EMB_D = 4096, 128, 512, 512, 128
C = 6.0 / np.sqrt(EMB_D)


def _partial_order_sim(hypers, hypos):
    act = np.maximum(hypers - hypos, 0.0)
    return -np.sqrt(np.sum(act * act, axis=-1))


def draw0():
    s, t = mx_kscale(VF_D), mx_kscale(HID_D)
    vfs = bf(np.random.standard_normal((B, VF_D)) * s)
    p_lfs = bf(np.random.standard_normal((B, EMB_D)) * 2.0 * C)
    n_lfs = bf(np.random.standard_normal((N, EMB_D)) * C)
    W_hidden = np.random.standard_normal((HID_D, VF_D)) / np.sqrt(VF_D) / s[None, :] * t[:, None]
    W_hidden_words, W_hidden_scales = pack4(W_hidden.T)
    b_hidden = bf(np.random.standard_normal(HID_D) * 0.5 * t)
    W_embed = np.random.standard_normal((EMB_D, HID_D)) * C / np.sqrt(HID_D) / t[None, :]
    W_embed_words, W_embed_scales = pack4(W_embed.T)
    b_embed = bf(np.random.standard_normal(EMB_D) * 0.5 * C)
    return {"vfs": vfs,
            "p_lfs": p_lfs,
            "n_lfs": n_lfs,
            "W_hidden_words": W_hidden_words,
            "W_hidden_scales": W_hidden_scales,
            "b_hidden": b_hidden,
            "W_embed_words": W_embed_words,
            "W_embed_scales": W_embed_scales,
            "b_embed": b_embed}


def core(vfs, p_lfs, n_lfs, W_hidden_words, W_hidden_scales, b_hidden, W_embed_words, W_embed_scales, b_embed):
    vf_hidden = (mxq(f64(vfs), 1, "e4m3") @ unpack4(W_hidden_words, W_hidden_scales)) + f64(b_hidden)
    vf_emb = (mxq(vf_hidden, 1, "e4m3") @ unpack4(W_embed_words, W_embed_scales)) + f64(b_embed)
    p_scores = _partial_order_sim(f64(p_lfs), vf_emb)
    n_scores = np.stack([_partial_order_sim(nl[None, :], vf_emb) for nl in f64(n_lfs)], axis=1)
    return np.concatenate([p_scores[:, None], n_scores], axis=1)


def e4m3fn_bytes(y):
    return np.clip(np.asarray(y, np.float64), -448.0, 448.0).astype(np.float32).astype(ml_dtypes.float8_e4m3fn).view(np.uint8)


def e4m3fn_values(b):
    return np.asarray(b, np.uint8).view(ml_dtypes.float8_e4m3fn).astype(np.float64)


def setup_inputs():
    d = draw0()
    x0 = np.asarray(d['vfs']).astype(np.float64)
    s = (np.max(np.abs(x0), axis=(0,), keepdims=True) / 448.0).astype(np.float32)
    out = {}
    for k, v in d.items():
        if k == 'vfs':
            out['vfs_bytes'] = e4m3fn_bytes(x0 / s.astype(np.float64))
            out['vfs_scale'] = s
        else:
            out[k] = v
    return out


def reference(vfs_bytes, vfs_scale, p_lfs, n_lfs, W_hidden_words, W_hidden_scales, b_hidden, W_embed_words, W_embed_scales, b_embed):
    return core(e4m3fn_values(vfs_bytes) * vfs_scale.astype(np.float64), p_lfs, n_lfs, W_hidden_words, W_hidden_scales, b_hidden, W_embed_words, W_embed_scales, b_embed)

@@ -1,0 +1,312 @@
+from contextlib import ExitStack
+
+import concourse.mybir as mybir
+from concourse.masks import make_identity
+
+B, K1, K2, D, J = 4096, 512, 512, 128, 128
+P = 128
+NT = B // P
+CT = 4
+NCHUNK = NT // CT
+W = CT * P
+FLOPS = 2 * B * (K1 * K2 + K2 * D) + 4 * B * (J + 1) * D
+
+F32 = mybir.dt.float32
+BF16 = mybir.dt.bfloat16
+I32 = mybir.dt.int32
+U32 = mybir.dt.uint32
+U8 = mybir.dt.uint8
+FP8 = mybir.dt.float8_e4m3fn
+FP8X4 = mybir.dt.float8_e4m3fn_x4
+FP4X4 = mybir.dt.float4_e2m1fn_x4
+ALU = mybir.AluOpType
+ACT = mybir.ActivationFunctionType
+
+NV = 36
+LA_R = 4
+LA_T = 2
+
+
+def tile_hypernymvisual_acc_t_w4_kernel(
+    tc, vfs_bytes, vfs_scale, p_lfs, n_lfs, W_hidden_words, W_hidden_scales, b_hidden, W_embed_words, W_embed_scales, b_embed, out
+):
+    nc = tc.nc
+    vb = vfs_bytes.rearrange("(p t) k -> p (t k)", t=NT)
+    pv = p_lfs.rearrange("(p t) d -> p t d", t=NT)
+    ov = out.rearrange("(p t) c -> p t c", t=NT)
+
+    with ExitStack() as ctx:
+        keep = ctx.enter_context(tc.tile_pool(name="keep", bufs=1))
+        stage = ctx.enter_context(tc.tile_pool(name="stage", bufs=2))
+        work = ctx.enter_context(tc.tile_pool(name="work", bufs=6))
+        psum = ctx.enter_context(tc.psum_pool(name="psum", bufs=2))
+        ctx.enter_context(tc.manual_schedule())
+
+        xb = []
+        for c in range(NCHUNK):
+            xbc = keep.tile([P, CT * K1], U8, name="xb%d" % c)
+            xb.append(xbc)
+        sc = keep.tile([P, K1], F32, name="sc")
+        nc.sync.dma_start(out=xb[0][:], in_=vb[:, 0 : CT * K1])
+        nc.sync.dma_start(out=sc[:], in_=vfs_scale.rearrange("o k -> (o k)").partition_broadcast(P))
+        whraw = keep.tile([P, 2 * K2], U8, name="whraw")
+        nc.sync.dma_start(out=whraw[:].bitcast(I32), in_=W_hidden_words[0].bitcast(I32))
+        we = keep.tile([P, 2 * D], U8, name="we", align_bytes=64)
+        nc.sync.dma_start(out=we[:].bitcast(I32), in_=W_embed_words[0].bitcast(I32))
+        whsraw = keep.tile([P, K2], U8, name="whsraw")
+        wes = keep.tile([P, D], U8, name="wes", align_bytes=64)
+        nc.vector.memset(whsraw[:].bitcast(I32), 0)
+        nc.vector.memset(wes[:].bitcast(I32), 0)
+        for q in range(4):
+            nc.sync.dma_start(out=whsraw[32 * q : 32 * q + 4, :].bitcast(I32), in_=W_hidden_scales[0, 4 * q : 4 * q + 4, :].bitcast(I32))
+        for q in range(4):
+            nc.sync.dma_start(out=wes[32 * q : 32 * q + 4, :].bitcast(I32), in_=W_embed_scales[0, 4 * q : 4 * q + 4, :].bitcast(I32))
+        bh = keep.tile([P, 4], BF16, name="bh")
+        nc.sync.dma_start(out=bh[:], in_=b_hidden.rearrange("(p t) -> p t", t=4))
+        be = keep.tile([P, 1], BF16, name="be")
+        nc.sync.dma_start(out=be[:], in_=b_embed.rearrange("(d o) -> d o", o=1))
+        nrow = keep.tile([P, D], BF16, name="nrow")
+        nc.sync.dma_start(out=nrow[:], in_=n_lfs)
+        for c in range(1, NCHUNK):
+            nc.sync.dma_start(out=xb[c][:], in_=vb[:, c * CT * K1 : (c + 1) * CT * K1])
+        pt = keep.tile([P, NT, D], BF16, name="pt")
+        nc.sync.dma_start(out=pt[:], in_=pv)
+
+        one = keep.tile([P, 1], F32, name="one")
+        nc.vector.memset(one[:], 1.0)
+        dummy = keep.tile([P, 1], F32, name="dummy")
+        nc.scalar.activation(out=dummy[:], in_=one[:], func=ACT.Sqrt)
+        ident = keep.tile([P, P], F32, name="ident")
+        make_identity(nc, ident[:])
+
+        wh = keep.tile([P, 2 * K2], U8, name="wh", align_bytes=64)
+        nc.vector.tensor_copy(
+            out=wh[:].rearrange("p (t m b) -> p t m b", t=4, b=2), in_=whraw[:].rearrange("p (m t b) -> p t m b", t=4, b=2)
+        )
+        whs = keep.tile([P, K2], U8, name="whs", align_bytes=64)
+        nc.vector.tensor_copy(out=whs[:].rearrange("p (t m) -> p t m", t=4), in_=whsraw[:].rearrange("p (m t) -> p t m", t=4))
+
+        n32 = keep.tile([P, D], F32, name="n32")
+        nT = keep.tile([P, J], F32, name="nT")
+
+        def prep_n():
+            nc.vector.tensor_copy(out=n32[:], in_=nrow[:])
+            pn = psum.tile([P, J], F32, name="pn", tag="pro", bufs=2)
+            nc.tensor.transpose(pn[:], n32[:], ident[:])
+            nc.vector.tensor_copy(out=nT[:], in_=pn[:])
+
+        eTs = {}
+        accs = {}
+        sts = {}
+
+        def prologue(c):
+            steps = []
+            xs = []
+            g = stage.tile([P, 4 * W], BF16, name="g", align_bytes=64)
+            cx = stage.tile([P, W], U32, name="cx", align_bytes=64)
+            sx = stage.tile([P, W], U8, name="sx", align_bytes=64)
+            h = stage.tile([P, 4 * W], BF16, name="h", align_bytes=64)
+            ch = stage.tile([P, W], U32, name="ch", align_bytes=64)
+            sh = stage.tile([P, W], U8, name="sh", align_bytes=64)
+            eT = stage.tile([P, W], F32, name="eT")
+            acc = stage.tile([P, CT, J + 1], F32, name="acc")
+            x = stage.tile([P, CT, D], F32, name="x")
+            x2 = stage.tile([P, CT, D], F32, name="x2")
+            eTs[c] = eT
+            accs[c] = acc
+            box = {}
+
+            def widen(a):
+                t = stage.tile([P, K1], BF16, name="xs", bufs=4)
+                nc.vector.tensor_tensor(out=t[:], in0=xb[c][:, a * K1 : (a + 1) * K1].bitcast(FP8), in1=sc[:], op=ALU.mult)
+                xs.append(t)
+
+            def turn(b):
+                px = psum.tile([P, 2, 2, P], F32, name="px", tag="pro", bufs=2)
+                for a in range(2):
+                    words = xs[2 * b + a][:].bitcast(F32)
+                    for u in range(2):
+                        nc.tensor.transpose(px[:, a, u, :], words[:, u : K1 // 2 : 2], ident[:])
+                box["px"] = px
+
+            def unload(b):
+                half = g[:].bitcast(F32)[:, b * W : (b + 1) * W]
+                nc.scalar.copy(
+                    out=half.rearrange("p (a r u) -> p a r u", a=2, u=2), in_=box["px"][:].rearrange("p a u r -> p a r u")
+                )
+
+            def quant_x():
+                nc.vector.quantize_mx(out=cx[:].bitcast(FP8X4), scales=sx[:], in_=g[:])
+
+            def mm1(a):
+                hp = psum.tile([P, 4, P], F32, name="hp", tag="pro", bufs=2)
+                cols = slice(a * P, (a + 1) * P)
+                for t in range(4):
+                    nc.tensor.matmul_mx(
+                        out=hp[:, t, :],
+                        lhsT=wh[:, 2 * P * t : 2 * P * (t + 1)].bitcast(FP4X4),
+                        lhsT_scale=whs[:, P * t : P * (t + 1)],
+                        rhs=cx[:, cols].bitcast(FP8X4),
+                        rhs_scale=sx[:, cols],
+                        start=True,
+                        stop=True,
+                    )
+                box["hp"] = hp
+
+            def bias1(a):
+                nc.vector.tensor_tensor(
+                    out=h[:, 4 * P * a : 4 * P * (a + 1)].rearrange("p (r t) -> p r t", t=4),
+                    in0=box["hp"][:].rearrange("p t r -> p r t"),
+                    in1=bh[:].unsqueeze(1).to_broadcast([P, P, 4]),
+                    op=ALU.add,
+                )
+
+            def quant_h():
+                nc.vector.quantize_mx(out=ch[:].bitcast(FP8X4), scales=sh[:], in_=h[:])
+
+            def mm2():
+                ep = psum.tile([P, W], F32, name="ep", tag="pro", bufs=2)
+                nc.tensor.matmul_mx(
+                    out=ep[:], lhsT=we[:].bitcast(FP4X4), lhsT_scale=wes[:], rhs=ch[:].bitcast(FP8X4), rhs_scale=sh[:], start=True, stop=True
+                )
+                box["ep"] = ep
+
+            def bias2():
+                nc.scalar.activation(out=eT[:], in_=box["ep"][:], func=ACT.Identity, bias=be[:, 0:1])
+
+            def turn_e():
+                pe = psum.tile([P, CT, D], F32, name="pe", tag="pro", bufs=2)
+                for a in range(CT):
+                    nc.tensor.transpose(pe[:, a, :], eT[:, a * P : (a + 1) * P], ident[:])
+                box["pe"] = pe
+
+            def pdiff():
+                nc.vector.tensor_tensor(out=x[:], in0=box["pe"][:], in1=pt[:, c * CT : (c + 1) * CT, :], op=ALU.subtract)
+
+            def prelu():
+                nc.vector.tensor_scalar(out=x2[:], in0=x[:], scalar1=0.0, scalar2=None, op0=ALU.min)
+
+            def psq():
+                jk = work.tile([P, CT, D], BF16, name="jk", bufs=3)
+                for a in range(CT):
+                    nc.scalar.activation(out=jk[:, a, :], in_=x2[:, a, :], func=ACT.Square, accum_out=acc[:, a, 0:1])
+
+            for a in range(4):
+                steps.append(lambda a=a: widen(a))
+            for b in range(2):
+                steps.append(lambda b=b: turn(b))
+                steps.append(lambda b=b: unload(b))
+            steps.append(quant_x)
+            for a in range(4):
+                steps.append(lambda a=a: mm1(a))
+                steps.append(lambda a=a: bias1(a))
+            steps.append(quant_h)
+            steps.append(mm2)
+            steps.append(bias2)
+            steps.append(turn_e)
+            steps.append(pdiff)
+            steps.append(prelu)
+            steps.append(psq)
+            return steps
+
+        def epilogue(c):
+            acc = accs[c]
+            st = sts[c]
+            o = stage.tile([P, CT * (J + 1)], F32, name="o")
+            o2 = stage.tile([P, CT, J + 1], F32, name="o2")
+            m2 = stage.tile([P, CT * NV, 2], F32, name="m2")
+            t2 = stage.tile([P, CT * NV, 2], F32, name="t2")
+            sv = st[:].rearrange("p a v (h s) -> p (a v) h s", h=2)
+
+            def post1():
+                nc.vector.tensor_tensor(out=m2[:], in0=sv[:, :, :, 1], in1=sv[:, :, :, 1], op=ALU.mult)
+
+            def post2():
+                nc.vector.scalar_tensor_tensor(out=t2[:], in0=m2[:], scalar=float(D // 2), in1=sv[:, :, :, 2], op0=ALU.mult, op1=ALU.add)
+
+            def post3():
+                tv = t2[:].rearrange("p (a v) h -> p a v h", a=CT)
+                nc.vector.tensor_tensor(out=acc[:, :, 1 + J - NV : 1 + J], in0=tv[:, :, :, 0], in1=tv[:, :, :, 1], op=ALU.add)
+
+            def root():
+                nc.scalar.activation(out=o[:], in_=acc[:].rearrange("p a c -> p (a c)"), func=ACT.Sqrt)
+
+            def neg():
+                nc.vector.tensor_scalar(out=o2[:].rearrange("p a c -> p (a c)"), in0=o[:], scalar1=-1.0, scalar2=None, op0=ALU.mult)
+
+            def store():
+                nc.sync.dma_start(out=ov[:, c * CT : (c + 1) * CT, :], in_=o2[:])
+
+            return [post1, post2, post3, root, neg, store]
+
+        units = []
+        for c in range(NCHUNK):
+            js = jv = 0
+            for k in range(J):
+                on_v = ((k + 1) * NV) // J > (k * NV) // J
+                if on_v:
+                    units.append((c, J - NV + jv, True, jv))
+                    jv += 1
+                else:
+                    units.append((c, js, False, -1))
+                    js += 1
+
+        rt = {}
+        pst = {}
+
+        def relu(n):
+            c, j, on_v, v = units[n]
+            r = work.tile([P, W], F32, name="r", bufs=6)
+            nc.vector.tensor_scalar(out=r[:], in0=eTs[c][:], scalar1=nT[:, j : j + 1], scalar2=0.0, op0=ALU.subtract, op1=ALU.min)
+            rt[n] = r
+
+        def turn_r(n):
+            c, j, on_v, v = units[n]
+            if on_v:
+                ps = psum.tile([P, CT, D], F32, name="psv", tag="psv", bufs=2)
+            else:
+                ps = psum.tile([P, CT, D], F32, name="pss", tag="pss", bufs=4)
+            r = rt.pop(n)
+            for a in range(CT):
+                nc.tensor.transpose(ps[:, a, :], r[:, a * P : (a + 1) * P], ident[:])
+            pst[n] = ps
+
+        def sumsq(n):
+            c, j, on_v, v = units[n]
+            ps = pst.pop(n)
+            if on_v:
+                if c not in sts:
+                    st = stage.tile([P, CT, NV, 6], F32, name="st")
+                    sts[c] = st
+                for a in range(CT):
+                    nc.vector.bn_stats(out=sts[c][:, a, v, :], in_=ps[:, a, :])
+            else:
+                jk = work.tile([P, CT, D], BF16, name="jk", bufs=3)
+                for a in range(CT):
+                    nc.scalar.activation(out=jk[:, a, :], in_=ps[:, a, :], func=ACT.Square, accum_out=accs[c][:, a, 1 + j : 2 + j])
+
+        prep_n()
+        for s in prologue(0):
+            s()
+
+        total = len(units)
+        extra = []
+        for n in range(-LA_R, total):
+            if n >= 0 and n % J == 0:
+                c = n // J
+                todo = []
+                if c > 0:
+                    todo += epilogue(c - 1)
+                if c + 1 < NCHUNK:
+                    todo += prologue(c + 1)
+                extra = [(n + 6 + (k * (J - 16)) // len(todo), f) for k, f in enumerate(todo)]
+            if n + LA_R < total and n + LA_R >= 0:
+                relu(n + LA_R)
+            if 0 <= n + LA_T < total:
+                turn_r(n + LA_T)
+            while extra and extra[0][0] <= n:
+                extra.pop(0)[1]()
+            if n >= 0:
+                sumsq(n)
+        for s in epilogue(NCHUNK - 1):
+            s()

@@ -21,10 +21,15 @@ FP8X4 = mybir.dt.float8_e4m3fn_x4
 FP4X4 = mybir.dt.float4_e2m1fn_x4
 ALU = mybir.AluOpType
 ACT = mybir.ActivationFunctionType
+AX = mybir.AxisListType
 
-NV = 36
-LA_R = 4
+NA = [0,4,0,4,0,4,3,0]
+LA_R = 5
 LA_T = 2
+A_FIRST = 30
+START = [0,0,70,105,195,230,325,372]
+PSS = 4
+SPACE = 1
 
 
 def tile_hypernymvisual_acc_t_w4_kernel(
@@ -38,16 +43,19 @@ def tile_hypernymvisual_acc_t_w4_kernel(
     with ExitStack() as ctx:
         keep = ctx.enter_context(tc.tile_pool(name="keep", bufs=1))
         stage = ctx.enter_context(tc.tile_pool(name="stage", bufs=2))
-        work = ctx.enter_context(tc.tile_pool(name="work", bufs=6))
-        psum = ctx.enter_context(tc.psum_pool(name="psum", bufs=2))
+        work = ctx.enter_context(tc.tile_pool(name="work", bufs=4))
+        psum = ctx.enter_context(tc.psum_pool(name="psum", bufs=1))
         ctx.enter_context(tc.manual_schedule())
 
-        xb = []
-        for c in range(NCHUNK):
-            xbc = keep.tile([P, CT * K1], U8, name="xb%d" % c)
-            xb.append(xbc)
+        xb = {}
+
+        def load_x(c):
+            xbc = stage.tile([P, CT * K1], U8, name="xbc", bufs=4)
+            nc.sync.dma_start(out=xbc[:], in_=vb[:, c * CT * K1 : (c + 1) * CT * K1])
+            xb[c] = xbc
+
+        load_x(0)
         sc = keep.tile([P, K1], F32, name="sc")
-        nc.sync.dma_start(out=xb[0][:], in_=vb[:, 0 : CT * K1])
         nc.sync.dma_start(out=sc[:], in_=vfs_scale.rearrange("o k -> (o k)").partition_broadcast(P))
         whraw = keep.tile([P, 2 * K2], U8, name="whraw")
         nc.sync.dma_start(out=whraw[:].bitcast(I32), in_=W_hidden_words[0].bitcast(I32))
@@ -67,10 +75,11 @@ def tile_hypernymvisual_acc_t_w4_kernel(
         nc.sync.dma_start(out=be[:], in_=b_embed.rearrange("(d o) -> d o", o=1))
         nrow = keep.tile([P, D], BF16, name="nrow")
         nc.sync.dma_start(out=nrow[:], in_=n_lfs)
-        for c in range(1, NCHUNK):
-            nc.sync.dma_start(out=xb[c][:], in_=vb[:, c * CT * K1 : (c + 1) * CT * K1])
+        load_x(1)
         pt = keep.tile([P, NT, D], BF16, name="pt")
         nc.sync.dma_start(out=pt[:], in_=pv)
+        for c in range(2, 4):
+            load_x(c)
 
         one = keep.tile([P, 1], F32, name="one")
         nc.vector.memset(one[:], 1.0)
@@ -88,33 +97,33 @@ def tile_hypernymvisual_acc_t_w4_kernel(
 
         n32 = keep.tile([P, D], F32, name="n32")
         nT = keep.tile([P, J], F32, name="nT")
-
-        def prep_n():
-            nc.vector.tensor_copy(out=n32[:], in_=nrow[:])
-            pn = psum.tile([P, J], F32, name="pn", tag="pro", bufs=2)
-            nc.tensor.transpose(pn[:], n32[:], ident[:])
-            nc.vector.tensor_copy(out=nT[:], in_=pn[:])
+        nTb = keep.tile([P, J], BF16, name="nTb")
+        nTneg = keep.tile([P, J], BF16, name="nTneg")
+        nc.vector.tensor_copy(out=n32[:], in_=nrow[:])
+        pn = psum.tile([P, J], F32, name="pn", tag="pro", bufs=1)
+        nc.tensor.transpose(pn[:], n32[:], ident[:])
+        nc.vector.tensor_copy(out=nT[:], in_=pn[:])
+        nc.vector.tensor_copy(out=nTb[:], in_=nT[:])
+        nc.vector.tensor_scalar(out=nTneg[:], in0=nT[:], scalar1=-1.0, scalar2=None, op0=ALU.mult)
 
         eTs = {}
         accs = {}
-        sts = {}
+        ehs = {}
+        v2s = {}
+        csts = {}
 
         def prologue(c):
             steps = []
             xs = []
-            g = stage.tile([P, 4 * W], BF16, name="g", align_bytes=64)
-            cx = stage.tile([P, W], U32, name="cx", align_bytes=64)
-            sx = stage.tile([P, W], U8, name="sx", align_bytes=64)
-            h = stage.tile([P, 4 * W], BF16, name="h", align_bytes=64)
-            ch = stage.tile([P, W], U32, name="ch", align_bytes=64)
-            sh = stage.tile([P, W], U8, name="sh", align_bytes=64)
-            eT = stage.tile([P, W], F32, name="eT")
-            acc = stage.tile([P, CT, J + 1], F32, name="acc")
-            x = stage.tile([P, CT, D], F32, name="x")
-            x2 = stage.tile([P, CT, D], F32, name="x2")
+            box = {}
+            eT = stage.tile([P, W], F32, name="eT", bufs=4)
+            acc = stage.tile([P, CT, J + 1], F32, name="acc", bufs=4)
             eTs[c] = eT
             accs[c] = acc
-            box = {}
+            if c == 0:
+                ptag = {"tag": "pss", "bufs": PSS}
+            else:
+                ptag = {"tag": "pro", "bufs": 1}
 
             def widen(a):
                 t = stage.tile([P, K1], BF16, name="xs", bufs=4)
@@ -122,52 +131,72 @@ def tile_hypernymvisual_acc_t_w4_kernel(
                 xs.append(t)
 
             def turn(b):
-                px = psum.tile([P, 2, 2, P], F32, name="px", tag="pro", bufs=2)
+                px = psum.tile([P, 2, 2, P], F32, name="px", **ptag)
                 for a in range(2):
                     words = xs[2 * b + a][:].bitcast(F32)
                     for u in range(2):
                         nc.tensor.transpose(px[:, a, u, :], words[:, u : K1 // 2 : 2], ident[:])
-                box["px"] = px
+                box["px%d" % b] = px
 
             def unload(b):
-                half = g[:].bitcast(F32)[:, b * W : (b + 1) * W]
+                if b == 0:
+                    g = stage.tile([P, 4 * W], BF16, name="g", align_bytes=64)
+                    box["g"] = g
+                half = box["g"][:].bitcast(F32)[:, b * W : (b + 1) * W]
                 nc.scalar.copy(
-                    out=half.rearrange("p (a r u) -> p a r u", a=2, u=2), in_=box["px"][:].rearrange("p a u r -> p a r u")
+                    out=half.rearrange("p (a r u) -> p a r u", a=2, u=2), in_=box["px%d" % b][:].rearrange("p a u r -> p a r u")
                 )
 
             def quant_x():
-                nc.vector.quantize_mx(out=cx[:].bitcast(FP8X4), scales=sx[:], in_=g[:])
+                cx = stage.tile([P, W], U32, name="cx", align_bytes=64)
+                sx = stage.tile([P, W], U8, name="sx", align_bytes=64)
+                nc.vector.quantize_mx(out=cx[:].bitcast(FP8X4), scales=sx[:], in_=box["g"][:])
+                box["cx"] = cx
+                box["sx"] = sx
 
             def mm1(a):
-                hp = psum.tile([P, 4, P], F32, name="hp", tag="pro", bufs=2)
+                hp = psum.tile([P, 4, P], F32, name="hp", **ptag)
                 cols = slice(a * P, (a + 1) * P)
                 for t in range(4):
                     nc.tensor.matmul_mx(
                         out=hp[:, t, :],
                         lhsT=wh[:, 2 * P * t : 2 * P * (t + 1)].bitcast(FP4X4),
                         lhsT_scale=whs[:, P * t : P * (t + 1)],
-                        rhs=cx[:, cols].bitcast(FP8X4),
-                        rhs_scale=sx[:, cols],
+                        rhs=box["cx"][:, cols].bitcast(FP8X4),
+                        rhs_scale=box["sx"][:, cols],
                         start=True,
                         stop=True,
                     )
-                box["hp"] = hp
+                box["hp%d" % a] = hp
 
             def bias1(a):
+                if a == 0:
+                    h = stage.tile([P, 4 * W], BF16, name="h", align_bytes=64)
+                    box["h"] = h
                 nc.vector.tensor_tensor(
-                    out=h[:, 4 * P * a : 4 * P * (a + 1)].rearrange("p (r t) -> p r t", t=4),
-                    in0=box["hp"][:].rearrange("p t r -> p r t"),
+                    out=box["h"][:, 4 * P * a : 4 * P * (a + 1)].rearrange("p (r t) -> p r t", t=4),
+                    in0=box["hp%d" % a][:].rearrange("p t r -> p r t"),
                     in1=bh[:].unsqueeze(1).to_broadcast([P, P, 4]),
                     op=ALU.add,
                 )
 
             def quant_h():
-                nc.vector.quantize_mx(out=ch[:].bitcast(FP8X4), scales=sh[:], in_=h[:])
+                ch = stage.tile([P, W], U32, name="ch", align_bytes=64)
+                sh = stage.tile([P, W], U8, name="sh", align_bytes=64)
+                nc.vector.quantize_mx(out=ch[:].bitcast(FP8X4), scales=sh[:], in_=box["h"][:])
+                box["ch"] = ch
+                box["sh"] = sh
 
             def mm2():
-                ep = psum.tile([P, W], F32, name="ep", tag="pro", bufs=2)
+                ep = psum.tile([P, W], F32, name="ep", **ptag)
                 nc.tensor.matmul_mx(
-                    out=ep[:], lhsT=we[:].bitcast(FP4X4), lhsT_scale=wes[:], rhs=ch[:].bitcast(FP8X4), rhs_scale=sh[:], start=True, stop=True
+                    out=ep[:],
+                    lhsT=we[:].bitcast(FP4X4),
+                    lhsT_scale=wes[:],
+                    rhs=box["ch"][:].bitcast(FP8X4),
+                    rhs_scale=box["sh"][:],
+                    start=True,
+                    stop=True,
                 )
                 box["ep"] = ep
 
@@ -175,27 +204,33 @@ def tile_hypernymvisual_acc_t_w4_kernel(
                 nc.scalar.activation(out=eT[:], in_=box["ep"][:], func=ACT.Identity, bias=be[:, 0:1])
 
             def turn_e():
-                pe = psum.tile([P, CT, D], F32, name="pe", tag="pro", bufs=2)
+                pe = psum.tile([P, CT, D], F32, name="pe", **ptag)
                 for a in range(CT):
                     nc.tensor.transpose(pe[:, a, :], eT[:, a * P : (a + 1) * P], ident[:])
                 box["pe"] = pe
 
             def pdiff():
+                x = stage.tile([P, CT, D], F32, name="x", bufs=1)
                 nc.vector.tensor_tensor(out=x[:], in0=box["pe"][:], in1=pt[:, c * CT : (c + 1) * CT, :], op=ALU.subtract)
+                box["x"] = x
 
             def prelu():
-                nc.vector.tensor_scalar(out=x2[:], in0=x[:], scalar1=0.0, scalar2=None, op0=ALU.min)
+                x2 = stage.tile([P, CT, D], F32, name="x2", bufs=1)
+                nc.vector.tensor_scalar(out=x2[:], in0=box["x"][:], scalar1=0.0, scalar2=None, op0=ALU.min)
+                box["x2"] = x2
 
             def psq():
                 jk = work.tile([P, CT, D], BF16, name="jk", bufs=3)
                 for a in range(CT):
-                    nc.scalar.activation(out=jk[:, a, :], in_=x2[:, a, :], func=ACT.Square, accum_out=acc[:, a, 0:1])
+                    nc.scalar.activation(out=jk[:, a, :], in_=box["x2"][:, a, :], func=ACT.Square, accum_out=acc[:, a, 0:1])
 
             for a in range(4):
                 steps.append(lambda a=a: widen(a))
             for b in range(2):
                 steps.append(lambda b=b: turn(b))
                 steps.append(lambda b=b: unload(b))
+            if c + 4 < NCHUNK:
+                steps.append(lambda: load_x(c + 4))
             steps.append(quant_x)
             for a in range(4):
                 steps.append(lambda a=a: mm1(a))
@@ -203,110 +238,284 @@ def tile_hypernymvisual_acc_t_w4_kernel(
             steps.append(quant_h)
             steps.append(mm2)
             steps.append(bias2)
-            steps.append(turn_e)
-            steps.append(pdiff)
-            steps.append(prelu)
-            steps.append(psq)
-            return steps
+            late = [turn_e, pdiff, prelu, psq]
+            na = NA[c]
+            if na:
+                wa = na * P
 
-        def epilogue(c):
-            acc = accs[c]
-            st = sts[c]
-            o = stage.tile([P, CT * (J + 1)], F32, name="o")
-            o2 = stage.tile([P, CT, J + 1], F32, name="o2")
-            m2 = stage.tile([P, CT * NV, 2], F32, name="m2")
-            t2 = stage.tile([P, CT * NV, 2], F32, name="t2")
-            sv = st[:].rearrange("p a v (h s) -> p (a v) h s", h=2)
+                def split1():
+                    eh = stage.tile([P, wa], BF16, name="eh")
+                    nc.vector.tensor_copy(out=eh[:], in_=eT[:, 0:wa])
+                    ehs[c] = eh
 
-            def post1():
-                nc.vector.tensor_tensor(out=m2[:], in0=sv[:, :, :, 1], in1=sv[:, :, :, 1], op=ALU.mult)
+                def split2():
+                    v2 = stage.tile([P, 2, wa], BF16, name="v2", bufs=3)
+                    w2 = stage.tile([P, wa], F32, name="w2", bufs=1)
+                    nc.vector.tensor_scalar(out=v2[:, 0, :], in0=ehs[c][:], scalar1=0.5, scalar2=None, op0=ALU.mult)
+                    nc.vector.scalar_tensor_tensor(out=v2[:, 1, :], in0=ehs[c][:], scalar=-1.0, in1=eT[:, 0:wa], op0=ALU.mult, op1=ALU.add)
+                    nc.vector.scalar_tensor_tensor(out=w2[:], in0=eT[:, 0:wa], scalar=2.0, in1=ehs[c][:], op0=ALU.mult, op1=ALU.subtract)
+                    v2s[c] = v2
+                    box["w2"] = w2
 
-            def post2():
-                nc.vector.scalar_tensor_tensor(out=t2[:], in0=m2[:], scalar=float(D // 2), in1=sv[:, :, :, 2], op0=ALU.mult, op1=ALU.add)
+                def split3():
+                    q2 = stage.tile([P, wa], F32, name="q2", bufs=1)
+                    nc.vector.tensor_tensor(out=q2[:], in0=box["w2"][:], in1=ehs[c][:], op=ALU.mult)
+                    box["q2"] = q2
 
-            def post3():
-                tv = t2[:].rearrange("p (a v) h -> p a v h", a=CT)
-                nc.vector.tensor_tensor(out=acc[:, :, 1 + J - NV : 1 + J], in0=tv[:, :, :, 0], in1=tv[:, :, :, 1], op=ALU.add)
+                def csum():
+                    pc = psum.tile([P, na], F32, name="pc", **ptag)
+                    for a in range(na):
+                        nc.tensor.matmul(pc[:, a : a + 1], lhsT=box["q2"][:, a * P : (a + 1) * P], rhs=one[:, 0:1], start=True, stop=True)
+                    box["pc"] = pc
+
+                def ccopy():
+                    cst = stage.tile([P, na], F32, name="cst", bufs=3)
+                    nc.vector.tensor_copy(out=cst[:], in_=box["pc"][:])
+                    csts[c] = cst
+
+                steps += [split1, split2, split3, csum, ccopy]
+            return steps + late
+
+
+        mas = {}
+        mbs = {}
+        psas = {}
+        psbs = {}
+        bTs = {}
+        tmps = {}
+
+        def max_j(c, j):
+            ma = work.tile([P, NA[c] * P], BF16, name="ma")
+            nc.vector.tensor_scalar(out=ma[:], in0=ehs[c][:], scalar1=nT[:, j : j + 1], scalar2=None, op0=ALU.max)
+            mas[c, j] = ma
+
+        def mul_n(c, j):
+            na = NA[c]
+            if j == 0:
+                psa = psum.tile([P, na, J], F32, name="psa", tag="psa", bufs=1)
+                psas[c] = psa
+            ma = mas.pop((c, j))
+            for a in range(na):
+                nc.tensor.matmul(psas[c][:, a, j : j + 1], lhsT=ma[:, a * P : (a + 1) * P], rhs=nTb[:, j : j + 1], start=True, stop=True)
+
+        def max_i(c, i0, ni):
+            mb = work.tile([P, ni, J], BF16, name="mb")
+            for k in range(ni):
+                nc.vector.tensor_scalar(out=mb[:, k, :], in0=nTb[:], scalar1=ehs[c][:, i0 + k : i0 + k + 1], scalar2=None, op0=ALU.max)
+            mbs[c, i0] = mb
+
+        def mul_e(c, i0, ni):
+            mb = mbs.pop((c, i0))
+            for k in range(ni):
+                i = i0 + k
+                pair, col = divmod(i, 2 * P)
+                if col == 0:
+                    psb = psum.tile([P, 2 * P, 2], F32, name="psb", tag="psb", bufs=2)
+                    psbs[c, pair] = psb
+                nc.tensor.matmul(psbs[c, pair][:, col, :], lhsT=mb[:, k, :], rhs=v2s[c][:, :, i], start=True, stop=True)
+
+        def fold(c, pair):
+            n = min(2 * P, NA[c] * P - 2 * P * pair)
+            if pair == 0:
+                bT = stage.tile([P, NA[c] * P], F32, name="bT", bufs=2)
+                bTs[c] = bT
+            nc.vector.tensor_reduce(out=bTs[c][:, 2 * P * pair : 2 * P * pair + n], in_=psbs[c, pair][:, 0:n, :], axis=AX.X, op=ALU.add)
+
+        def evac(c):
+            tmp = stage.tile([P, NA[c], J], F32, name="tmp", bufs=2)
+            for a in range(NA[c]):
+                nc.scalar.activation(out=tmp[:, a, :], in_=psas[c][:, a, :], func=ACT.Identity, bias=csts[c][:, a : a + 1])
+            tmps[c] = tmp
+
+        def combine(c):
+            na = NA[c]
+            box = {}
+
+            def bil():
+                pl = psum.tile([P, na, J], F32, name="pl", tag="pro", bufs=1)
+                for a in range(na):
+                    nc.tensor.matmul(pl[:, a, :], lhsT=ehs[c][:, a * P : (a + 1) * P], rhs=nTneg[:], start=True, stop=True)
+                box["pl"] = pl
+
+            def bil_add():
+                tmp2 = stage.tile([P, na, J], F32, name="tmp2", bufs=1)
+                nc.vector.tensor_tensor(out=tmp2[:], in0=box["pl"][:], in1=tmps[c][:], op=ALU.add)
+                box["tmp2"] = tmp2
+
+            def back():
+                pq = psum.tile([P, na, J], F32, name="pq", tag="pro", bufs=1)
+                for a in range(na):
+                    nc.tensor.transpose(pq[:, a, :], bTs[c][:, a * P : (a + 1) * P], ident[:])
+                box["pq"] = pq
+
+            def back_add():
+                tot = stage.tile([P, na, J], F32, name="tot", bufs=1)
+                nc.vector.scalar_tensor_tensor(out=tot[:], in0=box["pq"][:], scalar=-2.0, in1=box["tmp2"][:], op0=ALU.mult, op1=ALU.add)
+                box["tot"] = tot
+
+            def clamp():
+                nc.vector.tensor_scalar(out=accs[c][:, 0:na, 1 : 1 + J], in0=box["tot"][:], scalar1=0.0, scalar2=None, op0=ALU.max)
+
+            return [bil, bil_add, back, back_add, clamp]
+
+        def finish(c):
+            box = {}
 
             def root():
-                nc.scalar.activation(out=o[:], in_=acc[:].rearrange("p a c -> p (a c)"), func=ACT.Sqrt)
+                o = stage.tile([P, CT * (J + 1)], F32, name="o", bufs=1)
+                nc.scalar.activation(out=o[:], in_=accs[c][:].rearrange("p a c -> p (a c)"), func=ACT.Sqrt)
+                box["o"] = o
 
             def neg():
-                nc.vector.tensor_scalar(out=o2[:].rearrange("p a c -> p (a c)"), in0=o[:], scalar1=-1.0, scalar2=None, op0=ALU.mult)
-
-            def store():
+                o2 = stage.tile([P, CT, J + 1], F32, name="o2", bufs=2)
+                nc.vector.tensor_scalar(out=o2[:].rearrange("p a c -> p (a c)"), in0=box["o"][:], scalar1=-1.0, scalar2=None, op0=ALU.mult)
                 nc.sync.dma_start(out=ov[:, c * CT : (c + 1) * CT, :], in_=o2[:])
 
-            return [post1, post2, post3, root, neg, store]
+            return [root, neg]
 
         units = []
+        last = {}
         for c in range(NCHUNK):
-            js = jv = 0
-            for k in range(J):
-                on_v = ((k + 1) * NV) // J > (k * NV) // J
-                if on_v:
-                    units.append((c, J - NV + jv, True, jv))
-                    jv += 1
-                else:
-                    units.append((c, js, False, -1))
-                    js += 1
-
+            nd = CT - NA[c]
+            if nd:
+                jn = CT // nd
+                units += [(c, j, jn) for j in range(0, J, jn)]
+                last[c] = len(units) - 1
         rt = {}
         pst = {}
 
         def relu(n):
-            c, j, on_v, v = units[n]
-            r = work.tile([P, W], F32, name="r", bufs=6)
-            nc.vector.tensor_scalar(out=r[:], in0=eTs[c][:], scalar1=nT[:, j : j + 1], scalar2=0.0, op0=ALU.subtract, op1=ALU.min)
+            c, j, jn = units[n]
+            nd = CT - NA[c]
+            r = work.tile([P, jn, nd * P], F32, name="r", bufs=8)
+            for k in range(jn):
+                nc.vector.tensor_scalar(
+                    out=r[:, k, :], in0=eTs[c][:, NA[c] * P : W], scalar1=nT[:, j + k : j + k + 1], scalar2=0.0, op0=ALU.subtract, op1=ALU.min
+                )
             rt[n] = r
 
         def turn_r(n):
-            c, j, on_v, v = units[n]
-            if on_v:
-                ps = psum.tile([P, CT, D], F32, name="psv", tag="psv", bufs=2)
-            else:
-                ps = psum.tile([P, CT, D], F32, name="pss", tag="pss", bufs=4)
+            c, j, jn = units[n]
+            nd = CT - NA[c]
+            ps = psum.tile([P, jn, nd, D], F32, name="pss", tag="pss", bufs=PSS)
             r = rt.pop(n)
-            for a in range(CT):
-                nc.tensor.transpose(ps[:, a, :], r[:, a * P : (a + 1) * P], ident[:])
+            for k in range(jn):
+                for a in range(nd):
+                    nc.tensor.transpose(ps[:, k, a, :], r[:, k, a * P : (a + 1) * P], ident[:])
             pst[n] = ps
 
         def sumsq(n):
-            c, j, on_v, v = units[n]
+            c, j, jn = units[n]
+            na = NA[c]
+            nd = CT - na
             ps = pst.pop(n)
-            if on_v:
-                if c not in sts:
-                    st = stage.tile([P, CT, NV, 6], F32, name="st")
-                    sts[c] = st
-                for a in range(CT):
-                    nc.vector.bn_stats(out=sts[c][:, a, v, :], in_=ps[:, a, :])
-            else:
-                jk = work.tile([P, CT, D], BF16, name="jk", bufs=3)
-                for a in range(CT):
-                    nc.scalar.activation(out=jk[:, a, :], in_=ps[:, a, :], func=ACT.Square, accum_out=accs[c][:, a, 1 + j : 2 + j])
+            jk = work.tile([P, CT, D], BF16, name="jk", bufs=3)
+            for k in range(jn):
+                for a in range(nd):
+                    nc.scalar.activation(
+                        out=jk[:, k * nd + a, :], in_=ps[:, k, a, :], func=ACT.Square, accum_out=accs[c][:, na + a, 1 + j + k : 2 + j + k]
+                    )
 
-        prep_n()
+        steps_a = []
+        a_begin = {}
+        for c in range(NCHUNK):
+            if NA[c]:
+                a_begin[c] = len(steps_a)
+                ni = NA[c]
+                for s in range(J):
+                    steps_a.append((c, s, ni))
+        total = len(units)
+        n_a = len(steps_a)
+        done_a = 0
+        lag = 2
+        ready = set()
+        tasks = []
+        for c in range(NCHUNK):
+            tasks.append((START[c], c, "pro"))
+        queue = []
+        waiting = [c for c in range(NCHUNK) if c > 0]
+        fin = []
+
+        def a_step():
+            k = done_a
+            if k < n_a:
+                c, s, ni = steps_a[k]
+                max_j(c, s)
+                max_i(c, s * ni, ni)
+            if lag <= k < n_a + lag:
+                c, s, ni = steps_a[k - lag]
+                mul_n(c, s)
+                mul_e(c, s * ni, ni)
+                end = (s + 1) * ni
+                if end // (2 * P) > s * ni // (2 * P):
+                    fold_at.append((k + 1, c, s * ni // (2 * P)))
+                elif end == NA[c] * P:
+                    fold_at.append((k + 1, c, end // (2 * P)))
+                if s == J - 1:
+                    evac(c)
+                    fin.append((c, "a"))
+            while fold_at and fold_at[0][0] <= k:
+                q, c, pair = fold_at.pop(0)
+                fold(c, pair)
+
+        fold_at = []
         for s in prologue(0):
             s()
-
-        total = len(units)
-        extra = []
+        ready.add(0)
+        done_d = set()
+        done_aa = set(c for c in range(NCHUNK) if NA[c] == 0)
+        current = -1
         for n in range(-LA_R, total):
-            if n >= 0 and n % J == 0:
-                c = n // J
-                todo = []
-                if c > 0:
-                    todo += epilogue(c - 1)
-                if c + 1 < NCHUNK:
-                    todo += prologue(c + 1)
-                extra = [(n + 6 + (k * (J - 16)) // len(todo), f) for k, f in enumerate(todo)]
-            if n + LA_R < total and n + LA_R >= 0:
+            if n + LA_R < total:
+                assert units[n + LA_R][0] in ready
                 relu(n + LA_R)
             if 0 <= n + LA_T < total:
                 turn_r(n + LA_T)
-            while extra and extra[0][0] <= n:
-                extra.pop(0)[1]()
-            if n >= 0:
-                sumsq(n)
-        for s in epilogue(NCHUNK - 1):
-            s()
+            if n < 0:
+                continue
+            if not queue and waiting and n >= START[waiting[0]]:
+                current = waiting.pop(0)
+                queue = prologue(current)
+            elif not queue and fin:
+                c, kind = fin.pop(0)
+                if kind == "a":
+                    queue = combine(c)
+                    fin.insert(0, (c, "ac"))
+                elif kind == "ac":
+                    done_aa.add(c)
+                    if NA[c] == CT or c in done_d:
+                        queue = finish(c)
+                elif kind == "d":
+                    done_d.add(c)
+                    if c in done_aa:
+                        queue = finish(c)
+            if queue and n % SPACE == 0:
+                queue.pop(0)()
+                if not queue and current >= 0:
+                    ready.add(current)
+            goal = min(n_a + lag + 1, ((n - A_FIRST + 1) * (n_a + lag + 1)) // (total - A_FIRST - 16))
+            while done_a < goal:
+                if done_a < n_a:
+                    assert steps_a[done_a][0] in ready, (n, done_a)
+                a_step()
+                done_a += 1
+            sumsq(n)
+            c = units[n][0]
+            if last[c] == n:
+                fin.append((c, "d"))
+        while queue or fin:
+            if not queue:
+                c, kind = fin.pop(0)
+                if kind == "a":
+                    queue = combine(c)
+                    fin.insert(0, (c, "ac"))
+                elif kind == "ac":
+                    done_aa.add(c)
+                    if NA[c] == CT or c in done_d:
+                        queue = finish(c)
+                elif kind == "d":
+                    done_d.add(c)
+                    if c in done_aa:
+                        queue = finish(c)
+            else:
+                queue.pop(0)()

@@ -6,9 +6,9 @@ from concourse.masks import make_identity
 B, K1, K2, D, J = 4096, 512, 512, 128, 128
 P = 128
 NT = B // P
-CT = 4
-NCHUNK = NT // CT
-W = CT * P
+GT = 4
+W = GT * P
+PACK = 4
 FLOPS = 2 * B * (K1 * K2 + K2 * D) + 4 * B * (J + 1) * D
 
 F32 = mybir.dt.float32
@@ -23,499 +23,572 @@ ALU = mybir.AluOpType
 ACT = mybir.ActivationFunctionType
 AX = mybir.AxisListType
 
-NA = [0,4,0,4,0,4,3,0]
-LA_R = 5
-LA_T = 2
-A_FIRST = 30
-START = [0,0,70,105,195,230,325,372]
-PSS = 4
-SPACE = 1
+WAYS = ["TTTT", "DDDD", "PPPP", "TTTT", "PPPP", "TTTT", "PPPP", "PPPD"]
+NG = len(WAYS)
+
+RELU_AHEAD = 5
+TURN_AHEAD = 2
+PRODUCT_LAG = 4
+DIRECT_LAG = 3
+PAUSE = 2
+
+SCALAR_RELU = 4
+JD = 8
+EARLY = 30
+TAIL = 12
+
+INSTRUCTION = 24
+TASK = 220
 
 
 def tile_hypernymvisual_acc_t_w4_kernel(
     tc, vfs_bytes, vfs_scale, p_lfs, n_lfs, W_hidden_words, W_hidden_scales, b_hidden, W_embed_words, W_embed_scales, b_embed, out
 ):
     nc = tc.nc
-    vb = vfs_bytes.rearrange("(p t) k -> p (t k)", t=NT)
-    pv = p_lfs.rearrange("(p t) d -> p t d", t=NT)
-    ov = out.rearrange("(p t) c -> p t c", t=NT)
+    bytes_by_partition = vfs_bytes.rearrange("(p t) k -> p (t k)", t=NT)
+    positives_by_partition = p_lfs.rearrange("(p t) d -> p t d", t=NT)
+    out_by_partition = out.rearrange("(p t) c -> p t c", t=NT)
 
     with ExitStack() as ctx:
         keep = ctx.enter_context(tc.tile_pool(name="keep", bufs=1))
         stage = ctx.enter_context(tc.tile_pool(name="stage", bufs=2))
-        work = ctx.enter_context(tc.tile_pool(name="work", bufs=4))
+        work = ctx.enter_context(tc.tile_pool(name="work", bufs=2))
         psum = ctx.enter_context(tc.psum_pool(name="psum", bufs=1))
         ctx.enter_context(tc.manual_schedule())
 
-        xb = {}
+        code_bytes = {}
 
-        def load_x(c):
-            xbc = stage.tile([P, CT * K1], U8, name="xbc", bufs=4)
-            nc.sync.dma_start(out=xbc[:], in_=vb[:, c * CT * K1 : (c + 1) * CT * K1])
-            xb[c] = xbc
+        def load_bytes(g):
+            x_bytes = stage.tile([P, GT * K1], U8, name="x_bytes", bufs=4)
+            nc.sync.dma_start(out=x_bytes[:], in_=bytes_by_partition[:, g * GT * K1 : (g + 1) * GT * K1])
+            code_bytes[g] = x_bytes
 
-        load_x(0)
-        sc = keep.tile([P, K1], F32, name="sc")
-        nc.sync.dma_start(out=sc[:], in_=vfs_scale.rearrange("o k -> (o k)").partition_broadcast(P))
-        whraw = keep.tile([P, 2 * K2], U8, name="whraw")
-        nc.sync.dma_start(out=whraw[:].bitcast(I32), in_=W_hidden_words[0].bitcast(I32))
+        load_bytes(0)
+        x_scale = keep.tile([P, K1], F32, name="x_scale")
+        nc.sync.dma_start(out=x_scale[:], in_=vfs_scale.rearrange("o k -> (o k)").partition_broadcast(P))
+        wh_raw = keep.tile([P, 2 * K2], U8, name="wh_raw")
+        nc.sync.dma_start(out=wh_raw[:].bitcast(I32), in_=W_hidden_words[0].bitcast(I32))
         we = keep.tile([P, 2 * D], U8, name="we", align_bytes=64)
         nc.sync.dma_start(out=we[:].bitcast(I32), in_=W_embed_words[0].bitcast(I32))
-        whsraw = keep.tile([P, K2], U8, name="whsraw")
-        wes = keep.tile([P, D], U8, name="wes", align_bytes=64)
-        nc.vector.memset(whsraw[:].bitcast(I32), 0)
-        nc.vector.memset(wes[:].bitcast(I32), 0)
+        wh_scales_raw = keep.tile([P, K2], U8, name="wh_scales_raw")
+        we_scales = keep.tile([P, D], U8, name="we_scales", align_bytes=64)
+        nc.vector.memset(wh_scales_raw[:].bitcast(I32), 0)
+        nc.vector.memset(we_scales[:].bitcast(I32), 0)
         for q in range(4):
-            nc.sync.dma_start(out=whsraw[32 * q : 32 * q + 4, :].bitcast(I32), in_=W_hidden_scales[0, 4 * q : 4 * q + 4, :].bitcast(I32))
+            nc.sync.dma_start(
+                out=wh_scales_raw[32 * q : 32 * q + 4, :].bitcast(I32), in_=W_hidden_scales[0, 4 * q : 4 * q + 4, :].bitcast(I32)
+            )
         for q in range(4):
-            nc.sync.dma_start(out=wes[32 * q : 32 * q + 4, :].bitcast(I32), in_=W_embed_scales[0, 4 * q : 4 * q + 4, :].bitcast(I32))
-        bh = keep.tile([P, 4], BF16, name="bh")
-        nc.sync.dma_start(out=bh[:], in_=b_hidden.rearrange("(p t) -> p t", t=4))
-        be = keep.tile([P, 1], BF16, name="be")
-        nc.sync.dma_start(out=be[:], in_=b_embed.rearrange("(d o) -> d o", o=1))
-        nrow = keep.tile([P, D], BF16, name="nrow")
-        nc.sync.dma_start(out=nrow[:], in_=n_lfs)
-        load_x(1)
-        pt = keep.tile([P, NT, D], BF16, name="pt")
-        nc.sync.dma_start(out=pt[:], in_=pv)
-        for c in range(2, 4):
-            load_x(c)
+            nc.sync.dma_start(
+                out=we_scales[32 * q : 32 * q + 4, :].bitcast(I32), in_=W_embed_scales[0, 4 * q : 4 * q + 4, :].bitcast(I32)
+            )
+        bias_hidden = keep.tile([P, PACK], BF16, name="bias_hidden")
+        nc.sync.dma_start(out=bias_hidden[:], in_=b_hidden.rearrange("(p t) -> p t", t=PACK))
+        bias_embed = keep.tile([P, 1], BF16, name="bias_embed")
+        nc.sync.dma_start(out=bias_embed[:], in_=b_embed.rearrange("(d o) -> d o", o=1))
+        n_rows = keep.tile([P, D], BF16, name="n_rows")
+        nc.sync.dma_start(out=n_rows[:], in_=n_lfs)
+        load_bytes(1)
+        positives = keep.tile([P, NT, D], BF16, name="positives")
+        nc.sync.dma_start(out=positives[:], in_=positives_by_partition)
+        load_bytes(2)
+        load_bytes(3)
+        n_spread = keep.tile([P, J * D], BF16, name="n_spread")
+        nc.sync.dma_start(out=n_spread[:], in_=n_lfs.rearrange("j d -> (j d)").partition_broadcast(P))
 
         one = keep.tile([P, 1], F32, name="one")
         nc.vector.memset(one[:], 1.0)
-        dummy = keep.tile([P, 1], F32, name="dummy")
-        nc.scalar.activation(out=dummy[:], in_=one[:], func=ACT.Sqrt)
+        first_root = keep.tile([P, 1], F32, name="first_root")
+        nc.scalar.activation(out=first_root[:], in_=one[:], func=ACT.Sqrt)
         ident = keep.tile([P, P], F32, name="ident")
         make_identity(nc, ident[:])
 
         wh = keep.tile([P, 2 * K2], U8, name="wh", align_bytes=64)
-        nc.vector.tensor_copy(
-            out=wh[:].rearrange("p (t m b) -> p t m b", t=4, b=2), in_=whraw[:].rearrange("p (m t b) -> p t m b", t=4, b=2)
-        )
-        whs = keep.tile([P, K2], U8, name="whs", align_bytes=64)
-        nc.vector.tensor_copy(out=whs[:].rearrange("p (t m) -> p t m", t=4), in_=whsraw[:].rearrange("p (m t) -> p t m", t=4))
-
+        wh_scales = keep.tile([P, K2], U8, name="wh_scales", align_bytes=64)
         n32 = keep.tile([P, D], F32, name="n32")
         nT = keep.tile([P, J], F32, name="nT")
-        nTb = keep.tile([P, J], BF16, name="nTb")
-        nTneg = keep.tile([P, J], BF16, name="nTneg")
-        nc.vector.tensor_copy(out=n32[:], in_=nrow[:])
-        pn = psum.tile([P, J], F32, name="pn", tag="pro", bufs=1)
-        nc.tensor.transpose(pn[:], n32[:], ident[:])
-        nc.vector.tensor_copy(out=nT[:], in_=pn[:])
-        nc.vector.tensor_copy(out=nTb[:], in_=nT[:])
-        nc.vector.tensor_scalar(out=nTneg[:], in0=nT[:], scalar1=-1.0, scalar2=None, op0=ALU.mult)
+        nT_bf = keep.tile([P, J], BF16, name="nT_bf")
+        nT_minus = keep.tile([P, J], BF16, name="nT_minus")
 
-        eTs = {}
-        accs = {}
-        ehs = {}
-        v2s = {}
-        csts = {}
+        def arrange_weights():
+            nc.vector.tensor_copy(
+                out=wh[:].rearrange("p (t m b) -> p t m b", t=PACK, b=2), in_=wh_raw[:].rearrange("p (m t b) -> p t m b", t=PACK, b=2)
+            )
+            nc.vector.tensor_copy(
+                out=wh_scales[:].rearrange("p (t m) -> p t m", t=PACK), in_=wh_scales_raw[:].rearrange("p (m t) -> p t m", t=PACK)
+            )
 
-        def prologue(c):
-            steps = []
-            xs = []
+        def arrange_negatives():
+            nc.vector.tensor_copy(out=n32[:], in_=n_rows[:])
+            turned_n = psum.tile([P, J], F32, name="turned_n", tag="task", bufs=1)
+            nc.tensor.transpose(turned_n[:], n32[:], ident[:])
+            nc.vector.tensor_copy(out=nT[:], in_=turned_n[:])
+            nc.vector.tensor_copy(out=nT_bf[:], in_=nT[:])
+            nc.vector.tensor_scalar(out=nT_minus[:], in0=nT[:], scalar1=-1.0, scalar2=None, op0=ALU.mult)
+
+        eT = {}
+        e_rows = {}
+        e_high = {}
+        e_parts = {}
+        e_squares = {}
+        sums = {}
+        parts_done = {}
+        ended = []
+
+        def part_done(g):
+            parts_done[g] = parts_done.get(g, 0) + 1
+            if parts_done[g] == len(set(WAYS[g])):
+                ended.append((finish, g))
+
+        def pause():
+            pass
+
+        wait = [pause] * PAUSE
+
+        def square_sums(sources, targets):
+            squares = work.tile([P, len(sources), D], BF16, name="squares", bufs=3)
+            for k in range(len(sources)):
+                nc.scalar.activation(out=squares[:, k, :], in_=sources[k], func=ACT.Square, accum_out=targets[k])
+
+        def embed(g):
+            n_p = WAYS[g].count("P")
+            n_d = WAYS[g].count("D")
             box = {}
-            eT = stage.tile([P, W], F32, name="eT", bufs=4)
-            acc = stage.tile([P, CT, J + 1], F32, name="acc", bufs=4)
-            eTs[c] = eT
-            accs[c] = acc
-            if c == 0:
-                ptag = {"tag": "pss", "bufs": PSS}
-            else:
-                ptag = {"tag": "pro", "bufs": 1}
+            rows = []
+            eT_g = stage.tile([P, W], F32, name="eT_g", bufs=6)
+            sums_g = stage.tile([P, GT, 1 + J], F32, name="sums_g", bufs=NG)
+            eT[g] = eT_g
+            sums[g] = sums_g
+
+            def bank(name, shape):
+                if g == 0:
+                    return psum.tile(shape, F32, name=name, tag="turned", bufs=4)
+                return psum.tile(shape, F32, name=name, tag="task", bufs=1)
 
             def widen(a):
-                t = stage.tile([P, K1], BF16, name="xs", bufs=4)
-                nc.vector.tensor_tensor(out=t[:], in0=xb[c][:, a * K1 : (a + 1) * K1].bitcast(FP8), in1=sc[:], op=ALU.mult)
-                xs.append(t)
+                x = stage.tile([P, K1], BF16, name="x", bufs=4)
+                nc.vector.tensor_tensor(
+                    out=x[:], in0=code_bytes[g][:, a * K1 : (a + 1) * K1].bitcast(FP8), in1=x_scale[:], op=ALU.mult
+                )
+                rows.append(x)
 
-            def turn(b):
-                px = psum.tile([P, 2, 2, P], F32, name="px", **ptag)
+            def turn_x(b):
+                xT = bank("xT", [P, 2, 2, P])
                 for a in range(2):
-                    words = xs[2 * b + a][:].bitcast(F32)
+                    words = rows[2 * b + a][:].bitcast(F32)
                     for u in range(2):
-                        nc.tensor.transpose(px[:, a, u, :], words[:, u : K1 // 2 : 2], ident[:])
-                box["px%d" % b] = px
+                        nc.tensor.transpose(xT[:, a, u, :], words[:, u : K1 // 2 : 2], ident[:])
+                box["xT"] = xT
 
-            def unload(b):
+            def unload_x(b):
                 if b == 0:
-                    g = stage.tile([P, 4 * W], BF16, name="g", align_bytes=64)
-                    box["g"] = g
-                half = box["g"][:].bitcast(F32)[:, b * W : (b + 1) * W]
+                    x_packed = stage.tile([P, PACK * W], BF16, name="x_packed", align_bytes=64)
+                    box["x_packed"] = x_packed
+                half = box["x_packed"][:].bitcast(F32)[:, b * W : (b + 1) * W]
                 nc.scalar.copy(
-                    out=half.rearrange("p (a r u) -> p a r u", a=2, u=2), in_=box["px%d" % b][:].rearrange("p a u r -> p a r u")
+                    out=half.rearrange("p (a r u) -> p a r u", a=2, u=2), in_=box["xT"][:].rearrange("p a u r -> p a r u")
                 )
 
-            def quant_x():
-                cx = stage.tile([P, W], U32, name="cx", align_bytes=64)
-                sx = stage.tile([P, W], U8, name="sx", align_bytes=64)
-                nc.vector.quantize_mx(out=cx[:].bitcast(FP8X4), scales=sx[:], in_=box["g"][:])
-                box["cx"] = cx
-                box["sx"] = sx
+            def quantise_x():
+                x_codes = stage.tile([P, W], U32, name="x_codes", align_bytes=64)
+                x_scales = stage.tile([P, W], U8, name="x_scales", align_bytes=64)
+                nc.vector.quantize_mx(out=x_codes[:].bitcast(FP8X4), scales=x_scales[:], in_=box["x_packed"][:])
+                box["x_codes"] = x_codes
+                box["x_scales"] = x_scales
 
-            def mm1(a):
-                hp = psum.tile([P, 4, P], F32, name="hp", **ptag)
+            def multiply_x(a):
+                hT = bank("hT", [P, PACK, P])
                 cols = slice(a * P, (a + 1) * P)
-                for t in range(4):
+                for t in range(PACK):
                     nc.tensor.matmul_mx(
-                        out=hp[:, t, :],
+                        out=hT[:, t, :],
                         lhsT=wh[:, 2 * P * t : 2 * P * (t + 1)].bitcast(FP4X4),
-                        lhsT_scale=whs[:, P * t : P * (t + 1)],
-                        rhs=box["cx"][:, cols].bitcast(FP8X4),
-                        rhs_scale=box["sx"][:, cols],
+                        lhsT_scale=wh_scales[:, P * t : P * (t + 1)],
+                        rhs=box["x_codes"][:, cols].bitcast(FP8X4),
+                        rhs_scale=box["x_scales"][:, cols],
                         start=True,
                         stop=True,
                     )
-                box["hp%d" % a] = hp
+                box["hT"] = hT
 
-            def bias1(a):
+            def add_bias(a):
                 if a == 0:
-                    h = stage.tile([P, 4 * W], BF16, name="h", align_bytes=64)
-                    box["h"] = h
+                    h_packed = stage.tile([P, PACK * W], BF16, name="h_packed", align_bytes=64)
+                    box["h_packed"] = h_packed
                 nc.vector.tensor_tensor(
-                    out=box["h"][:, 4 * P * a : 4 * P * (a + 1)].rearrange("p (r t) -> p r t", t=4),
-                    in0=box["hp%d" % a][:].rearrange("p t r -> p r t"),
-                    in1=bh[:].unsqueeze(1).to_broadcast([P, P, 4]),
+                    out=box["h_packed"][:, PACK * P * a : PACK * P * (a + 1)].rearrange("p (r t) -> p r t", t=PACK),
+                    in0=box["hT"][:].rearrange("p t r -> p r t"),
+                    in1=bias_hidden[:].unsqueeze(1).to_broadcast([P, P, PACK]),
                     op=ALU.add,
                 )
 
-            def quant_h():
-                ch = stage.tile([P, W], U32, name="ch", align_bytes=64)
-                sh = stage.tile([P, W], U8, name="sh", align_bytes=64)
-                nc.vector.quantize_mx(out=ch[:].bitcast(FP8X4), scales=sh[:], in_=box["h"][:])
-                box["ch"] = ch
-                box["sh"] = sh
+            def quantise_h():
+                h_codes = stage.tile([P, W], U32, name="h_codes", align_bytes=64)
+                h_scales = stage.tile([P, W], U8, name="h_scales", align_bytes=64)
+                nc.vector.quantize_mx(out=h_codes[:].bitcast(FP8X4), scales=h_scales[:], in_=box["h_packed"][:])
+                box["h_codes"] = h_codes
+                box["h_scales"] = h_scales
 
-            def mm2():
-                ep = psum.tile([P, W], F32, name="ep", **ptag)
+            def multiply_h():
+                raw_eT = bank("raw_eT", [P, W])
                 nc.tensor.matmul_mx(
-                    out=ep[:],
+                    out=raw_eT[:],
                     lhsT=we[:].bitcast(FP4X4),
-                    lhsT_scale=wes[:],
-                    rhs=box["ch"][:].bitcast(FP8X4),
-                    rhs_scale=box["sh"][:],
+                    lhsT_scale=we_scales[:],
+                    rhs=box["h_codes"][:].bitcast(FP8X4),
+                    rhs_scale=box["h_scales"][:],
                     start=True,
                     stop=True,
                 )
-                box["ep"] = ep
+                box["raw_eT"] = raw_eT
 
-            def bias2():
-                nc.scalar.activation(out=eT[:], in_=box["ep"][:], func=ACT.Identity, bias=be[:, 0:1])
+            def unload_e():
+                nc.scalar.activation(out=eT_g[:], in_=box["raw_eT"][:], func=ACT.Identity, bias=bias_embed[:, 0:1])
 
             def turn_e():
-                pe = psum.tile([P, CT, D], F32, name="pe", **ptag)
-                for a in range(CT):
-                    nc.tensor.transpose(pe[:, a, :], eT[:, a * P : (a + 1) * P], ident[:])
-                box["pe"] = pe
+                e_bank = bank("e_bank", [P, GT, D])
+                for a in range(GT):
+                    nc.tensor.transpose(e_bank[:, a, :], eT_g[:, a * P : (a + 1) * P], ident[:])
+                box["e_bank"] = e_bank
 
-            def pdiff():
-                x = stage.tile([P, CT, D], F32, name="x", bufs=1)
-                nc.vector.tensor_tensor(out=x[:], in0=box["pe"][:], in1=pt[:, c * CT : (c + 1) * CT, :], op=ALU.subtract)
-                box["x"] = x
+            def positive_difference():
+                x_pos = stage.tile([P, GT, D], F32, name="x_pos", bufs=1)
+                nc.vector.tensor_tensor(
+                    out=x_pos[:], in0=box["e_bank"][:], in1=positives[:, g * GT : (g + 1) * GT, :], op=ALU.subtract
+                )
+                box["x_pos"] = x_pos
 
-            def prelu():
-                x2 = stage.tile([P, CT, D], F32, name="x2", bufs=1)
-                nc.vector.tensor_scalar(out=x2[:], in0=box["x"][:], scalar1=0.0, scalar2=None, op0=ALU.min)
-                box["x2"] = x2
+            def keep_e_rows():
+                if n_p:
+                    e_squares_g = stage.tile([P, n_p], F32, name="e_squares_g", bufs=3)
+                    square_sums([box["e_bank"][:, a, :] for a in range(n_p)], [e_squares_g[:, a : a + 1] for a in range(n_p)])
+                    e_squares[g] = e_squares_g
+                if n_d:
+                    e_rows_g = stage.tile([P, n_d, D], F32, name="e_rows_g", bufs=2)
+                    nc.scalar.copy(out=e_rows_g[:], in_=box["e_bank"][:, GT - n_d : GT, :])
+                    e_rows[g] = e_rows_g
 
-            def psq():
-                jk = work.tile([P, CT, D], BF16, name="jk", bufs=3)
-                for a in range(CT):
-                    nc.scalar.activation(out=jk[:, a, :], in_=box["x2"][:, a, :], func=ACT.Square, accum_out=acc[:, a, 0:1])
+            def positive_relu():
+                r_pos = stage.tile([P, GT, D], F32, name="r_pos", bufs=1)
+                nc.vector.tensor_scalar(out=r_pos[:], in0=box["x_pos"][:], scalar1=0.0, scalar2=None, op0=ALU.min)
+                box["r_pos"] = r_pos
 
-            for a in range(4):
-                steps.append(lambda a=a: widen(a))
+            def positive_sums():
+                square_sums([box["r_pos"][:, a, :] for a in range(GT)], [sums_g[:, a, 0:1] for a in range(GT)])
+
+            def split_e():
+                e_high_g = stage.tile([P, n_p * P], BF16, name="e_high_g", bufs=3)
+                e_parts_g = stage.tile([P, 2, n_p * P], BF16, name="e_parts_g", bufs=3)
+                e_p = eT_g[:, 0 : n_p * P]
+                nc.vector.tensor_copy(out=e_high_g[:], in_=e_p)
+                nc.vector.tensor_scalar(out=e_parts_g[:, 0, :], in0=e_high_g[:], scalar1=0.5, scalar2=None, op0=ALU.mult)
+                nc.vector.scalar_tensor_tensor(
+                    out=e_parts_g[:, 1, :], in0=e_high_g[:], scalar=-1.0, in1=e_p, op0=ALU.mult, op1=ALU.add
+                )
+                e_high[g] = e_high_g
+                e_parts[g] = e_parts_g
+
+            tasks = [lambda a=a: widen(a) for a in range(GT)]
             for b in range(2):
-                steps.append(lambda b=b: turn(b))
-                steps.append(lambda b=b: unload(b))
-            if c + 4 < NCHUNK:
-                steps.append(lambda: load_x(c + 4))
-            steps.append(quant_x)
-            for a in range(4):
-                steps.append(lambda a=a: mm1(a))
-                steps.append(lambda a=a: bias1(a))
-            steps.append(quant_h)
-            steps.append(mm2)
-            steps.append(bias2)
-            late = [turn_e, pdiff, prelu, psq]
-            na = NA[c]
-            if na:
-                wa = na * P
+                tasks += [lambda b=b: turn_x(b)] + wait + [lambda b=b: unload_x(b)]
+            if g + 4 < NG:
+                tasks.append(lambda: load_bytes(g + 4))
+            if g == 0:
+                tasks += [arrange_weights, arrange_negatives]
+            tasks += wait + [quantise_x] + wait
+            for a in range(GT):
+                tasks += [lambda a=a: multiply_x(a)] + wait + [lambda a=a: add_bias(a)]
+            tasks += [quantise_h] + wait + [multiply_h] + wait + [unload_e] + wait
+            tasks += [turn_e] + wait + [positive_difference, keep_e_rows, positive_relu] + wait + [positive_sums]
+            if n_p:
+                tasks.append(split_e)
+            return tasks
 
-                def split1():
-                    eh = stage.tile([P, wa], BF16, name="eh")
-                    nc.vector.tensor_copy(out=eh[:], in_=eT[:, 0:wa])
-                    ehs[c] = eh
+        m_rows = {}
+        m_negatives = {}
+        m_n = {}
+        m_e = {}
+        m_e_sums = {}
+        m_n_sums = {}
 
-                def split2():
-                    v2 = stage.tile([P, 2, wa], BF16, name="v2", bufs=3)
-                    w2 = stage.tile([P, wa], F32, name="w2", bufs=1)
-                    nc.vector.tensor_scalar(out=v2[:, 0, :], in0=ehs[c][:], scalar1=0.5, scalar2=None, op0=ALU.mult)
-                    nc.vector.scalar_tensor_tensor(out=v2[:, 1, :], in0=ehs[c][:], scalar=-1.0, in1=eT[:, 0:wa], op0=ALU.mult, op1=ALU.add)
-                    nc.vector.scalar_tensor_tensor(out=w2[:], in0=eT[:, 0:wa], scalar=2.0, in1=ehs[c][:], op0=ALU.mult, op1=ALU.subtract)
-                    v2s[c] = v2
-                    box["w2"] = w2
+        def make_m_rows(g, j):
+            m_row = work.tile([P, WAYS[g].count("P") * P], BF16, name="m_row", bufs=PRODUCT_LAG + 3)
+            nc.vector.tensor_scalar(out=m_row[:], in0=e_high[g][:], scalar1=nT[:, j : j + 1], scalar2=None, op0=ALU.max)
+            m_rows[g, j] = m_row
 
-                def split3():
-                    q2 = stage.tile([P, wa], F32, name="q2", bufs=1)
-                    nc.vector.tensor_tensor(out=q2[:], in0=box["w2"][:], in1=ehs[c][:], op=ALU.mult)
-                    box["q2"] = q2
-
-                def csum():
-                    pc = psum.tile([P, na], F32, name="pc", **ptag)
-                    for a in range(na):
-                        nc.tensor.matmul(pc[:, a : a + 1], lhsT=box["q2"][:, a * P : (a + 1) * P], rhs=one[:, 0:1], start=True, stop=True)
-                    box["pc"] = pc
-
-                def ccopy():
-                    cst = stage.tile([P, na], F32, name="cst", bufs=3)
-                    nc.vector.tensor_copy(out=cst[:], in_=box["pc"][:])
-                    csts[c] = cst
-
-                steps += [split1, split2, split3, csum, ccopy]
-            return steps + late
-
-
-        mas = {}
-        mbs = {}
-        psas = {}
-        psbs = {}
-        bTs = {}
-        tmps = {}
-
-        def max_j(c, j):
-            ma = work.tile([P, NA[c] * P], BF16, name="ma")
-            nc.vector.tensor_scalar(out=ma[:], in0=ehs[c][:], scalar1=nT[:, j : j + 1], scalar2=None, op0=ALU.max)
-            mas[c, j] = ma
-
-        def mul_n(c, j):
-            na = NA[c]
+        def multiply_n(g, j):
+            n_p = WAYS[g].count("P")
             if j == 0:
-                psa = psum.tile([P, na, J], F32, name="psa", tag="psa", bufs=1)
-                psas[c] = psa
-            ma = mas.pop((c, j))
-            for a in range(na):
-                nc.tensor.matmul(psas[c][:, a, j : j + 1], lhsT=ma[:, a * P : (a + 1) * P], rhs=nTb[:, j : j + 1], start=True, stop=True)
+                m_n_bank = psum.tile([P, n_p, J], F32, name="m_n_bank", tag="m_n", bufs=1)
+                m_n[g] = m_n_bank
+            m_row = m_rows.pop((g, j))
+            for a in range(n_p):
+                nc.tensor.matmul(
+                    m_n[g][:, a, j : j + 1], lhsT=m_row[:, a * P : (a + 1) * P], rhs=nT_bf[:, j : j + 1], start=True, stop=True
+                )
 
-        def max_i(c, i0, ni):
-            mb = work.tile([P, ni, J], BF16, name="mb")
+        def make_m_negatives(g, i0, ni):
+            m_negative = work.tile([P, ni, J], BF16, name="m_negative", bufs=PRODUCT_LAG + 3)
             for k in range(ni):
-                nc.vector.tensor_scalar(out=mb[:, k, :], in0=nTb[:], scalar1=ehs[c][:, i0 + k : i0 + k + 1], scalar2=None, op0=ALU.max)
-            mbs[c, i0] = mb
+                nc.vector.tensor_scalar(
+                    out=m_negative[:, k, :], in0=nT_bf[:], scalar1=e_high[g][:, i0 + k : i0 + k + 1], scalar2=None, op0=ALU.max
+                )
+            m_negatives[g, i0] = m_negative
 
-        def mul_e(c, i0, ni):
-            mb = mbs.pop((c, i0))
+        def multiply_e(g, i0, ni):
+            m_negative = m_negatives.pop((g, i0))
             for k in range(ni):
-                i = i0 + k
-                pair, col = divmod(i, 2 * P)
+                half, col = divmod(i0 + k, 2 * P)
                 if col == 0:
-                    psb = psum.tile([P, 2 * P, 2], F32, name="psb", tag="psb", bufs=2)
-                    psbs[c, pair] = psb
-                nc.tensor.matmul(psbs[c, pair][:, col, :], lhsT=mb[:, k, :], rhs=v2s[c][:, :, i], start=True, stop=True)
+                    m_e_bank = psum.tile([P, 2 * P, 2], F32, name="m_e_bank", tag="m_e", bufs=2)
+                    m_e[g, half] = m_e_bank
+                nc.tensor.matmul(
+                    m_e[g, half][:, col, :], lhsT=m_negative[:, k, :], rhs=e_parts[g][:, :, i0 + k], start=True, stop=True
+                )
 
-        def fold(c, pair):
-            n = min(2 * P, NA[c] * P - 2 * P * pair)
-            if pair == 0:
-                bT = stage.tile([P, NA[c] * P], F32, name="bT", bufs=2)
-                bTs[c] = bT
-            nc.vector.tensor_reduce(out=bTs[c][:, 2 * P * pair : 2 * P * pair + n], in_=psbs[c, pair][:, 0:n, :], axis=AX.X, op=ALU.add)
+        def fold(g, half):
+            n_rows_p = WAYS[g].count("P") * P
+            begin, end = 2 * P * half, min(2 * P * (half + 1), n_rows_p)
+            if half == 0:
+                m_e_sum = stage.tile([P, n_rows_p], F32, name="m_e_sum")
+                m_e_sums[g] = m_e_sum
+            nc.vector.tensor_reduce(out=m_e_sums[g][:, begin:end], in_=m_e[g, half][:, 0 : end - begin, :], axis=AX.X, op=ALU.add)
 
-        def evac(c):
-            tmp = stage.tile([P, NA[c], J], F32, name="tmp", bufs=2)
-            for a in range(NA[c]):
-                nc.scalar.activation(out=tmp[:, a, :], in_=psas[c][:, a, :], func=ACT.Identity, bias=csts[c][:, a : a + 1])
-            tmps[c] = tmp
+        def unload_m_n(g):
+            n_p = WAYS[g].count("P")
+            m_n_sum = stage.tile([P, n_p, J], F32, name="m_n_sum")
+            for a in range(n_p):
+                nc.scalar.activation(out=m_n_sum[:, a, :], in_=m_n[g][:, a, :], func=ACT.Identity, bias=e_squares[g][:, a : a + 1])
+            m_n_sums[g] = m_n_sum
 
-        def combine(c):
-            na = NA[c]
+        def combine(g):
+            n_p = WAYS[g].count("P")
             box = {}
 
-            def bil():
-                pl = psum.tile([P, na, J], F32, name="pl", tag="pro", bufs=1)
-                for a in range(na):
-                    nc.tensor.matmul(pl[:, a, :], lhsT=ehs[c][:, a * P : (a + 1) * P], rhs=nTneg[:], start=True, stop=True)
-                box["pl"] = pl
+            def multiply_n_eh():
+                n_eh = psum.tile([P, n_p, J], F32, name="n_eh", tag="task", bufs=1)
+                for a in range(n_p):
+                    nc.tensor.matmul(n_eh[:, a, :], lhsT=e_high[g][:, a * P : (a + 1) * P], rhs=nT_minus[:], start=True, stop=True)
+                box["n_eh"] = n_eh
 
-            def bil_add():
-                tmp2 = stage.tile([P, na, J], F32, name="tmp2", bufs=1)
-                nc.vector.tensor_tensor(out=tmp2[:], in0=box["pl"][:], in1=tmps[c][:], op=ALU.add)
-                box["tmp2"] = tmp2
+            def add_n_eh():
+                without_m_e = stage.tile([P, n_p, J], F32, name="without_m_e", bufs=1)
+                nc.vector.tensor_tensor(out=without_m_e[:], in0=box["n_eh"][:], in1=m_n_sums[g][:], op=ALU.add)
+                box["without_m_e"] = without_m_e
 
-            def back():
-                pq = psum.tile([P, na, J], F32, name="pq", tag="pro", bufs=1)
-                for a in range(na):
-                    nc.tensor.transpose(pq[:, a, :], bTs[c][:, a * P : (a + 1) * P], ident[:])
-                box["pq"] = pq
+            def turn_m_e():
+                m_e_turned = psum.tile([P, n_p, J], F32, name="m_e_turned", tag="task", bufs=1)
+                for a in range(n_p):
+                    nc.tensor.transpose(m_e_turned[:, a, :], m_e_sums[g][:, a * P : (a + 1) * P], ident[:])
+                box["m_e_turned"] = m_e_turned
 
-            def back_add():
-                tot = stage.tile([P, na, J], F32, name="tot", bufs=1)
-                nc.vector.scalar_tensor_tensor(out=tot[:], in0=box["pq"][:], scalar=-2.0, in1=box["tmp2"][:], op0=ALU.mult, op1=ALU.add)
-                box["tot"] = tot
+            def add_m_e():
+                total = stage.tile([P, n_p, J], F32, name="total", bufs=1)
+                nc.vector.scalar_tensor_tensor(
+                    out=total[:], in0=box["m_e_turned"][:], scalar=-2.0, in1=box["without_m_e"][:], op0=ALU.mult, op1=ALU.add
+                )
+                box["total"] = total
 
-            def clamp():
-                nc.vector.tensor_scalar(out=accs[c][:, 0:na, 1 : 1 + J], in0=box["tot"][:], scalar1=0.0, scalar2=None, op0=ALU.max)
+            def clip():
+                nc.vector.tensor_scalar(out=sums[g][:, 0:n_p, 1 : 1 + J], in0=box["total"][:], scalar1=0.0, scalar2=None, op0=ALU.max)
+                part_done(g)
 
-            return [bil, bil_add, back, back_add, clamp]
+            return [multiply_n_eh] + wait + [add_n_eh, turn_m_e] + wait + [add_m_e, clip]
 
-        def finish(c):
+        product_steps = [(g, s, WAYS[g].count("P")) for g in range(NG) if "P" in WAYS[g] for s in range(J)]
+        folds = []
+
+        def product_step(k):
+            if k < len(product_steps):
+                g, s, ni = product_steps[k]
+                make_m_rows(g, s)
+                make_m_negatives(g, s * ni, ni)
+            if PRODUCT_LAG <= k < len(product_steps) + PRODUCT_LAG:
+                g, s, ni = product_steps[k - PRODUCT_LAG]
+                multiply_n(g, s)
+                multiply_e(g, s * ni, ni)
+                half, end = s * ni // (2 * P), (s + 1) * ni
+                last = end == ni * P
+                if end // (2 * P) > half or last:
+                    folds.append((k + 1, g, half, last))
+                if s == J - 1:
+                    unload_m_n(g)
+            while folds and folds[0][0] <= k:
+                after, g, half, last = folds.pop(0)
+                fold(g, half)
+                if last:
+                    ended.append((combine, g))
+
+        def product_weight(k):
+            g, s, ni = product_steps[min(k, len(product_steps) - 1)]
+            return INSTRUCTION * (1 + ni) + ni * P // 4 + ni * J // 4
+
+        direct_steps = [(g, a, q) for g in range(NG) for a in range(WAYS[g].count("D")) for q in range(J // JD)]
+        direct_relus = {}
+        unclipped = []
+
+        def direct_difference(g, a, q):
+            x_dir = work.tile([P, JD, D], F32, name="x_dir")
+            r_dir = work.tile([P, JD * D], F32, name="r_dir", bufs=4)
+            nc.vector.tensor_tensor(
+                out=x_dir[:],
+                in0=n_spread[:, q * JD * D : (q + 1) * JD * D].rearrange("p (j d) -> p j d", d=D),
+                in1=e_rows[g][:, a : a + 1, :].to_broadcast([P, JD, D]),
+                op=ALU.subtract,
+            )
+            direct_relus[g, a, q] = r_dir
+            unclipped.append((x_dir, r_dir))
+
+        def direct_relu():
+            x_dir, r_dir = unclipped.pop(0)
+            nc.vector.tensor_scalar(out=r_dir[:], in0=x_dir[:].rearrange("p j d -> p (j d)"), scalar1=0.0, scalar2=None, op0=ALU.max)
+
+        def direct_sums(g, a, q, k0):
+            tile = GT - WAYS[g].count("D") + a
+            ks = range(k0, k0 + 2)
+            square_sums(
+                [direct_relus[g, a, q][:, k * D : (k + 1) * D] for k in ks],
+                [sums[g][:, tile, 1 + q * JD + k : 2 + q * JD + k] for k in ks],
+            )
+            if (a + 1, q + 1, k0 + 2) == (WAYS[g].count("D"), J // JD, JD):
+                part_done(g)
+
+        direct_weight = 2 * INSTRUCTION + JD * D + JD * D // 2
+
+        units = [(g, j) for g in range(NG) if WAYS[g] == "TTTT" for j in range(J)]
+        turned_relus = {}
+        turned_banks = {}
+
+        def on_scalar(n):
+            return n % SCALAR_RELU == SCALAR_RELU - 1
+
+        def turned_relu(n):
+            g, j = units[n]
+            r = work.tile([P, W], F32, name="r", bufs=8)
+            if on_scalar(n):
+                nc.scalar.activation(out=r[:], in_=eT[g][:], func=ACT.Relu, scale=-1.0, bias=nT[:, j : j + 1])
+            else:
+                nc.vector.tensor_scalar(out=r[:], in0=eT[g][:], scalar1=nT[:, j : j + 1], scalar2=0.0, op0=ALU.subtract, op1=ALU.min)
+            turned_relus[n] = r
+
+        def turn_relu(n):
+            r_bank = psum.tile([P, GT, D], F32, name="r_bank", tag="turned", bufs=4)
+            r = turned_relus.pop(n)
+            for a in range(GT):
+                nc.tensor.transpose(r_bank[:, a, :], r[:, a * P : (a + 1) * P], ident[:])
+            turned_banks[n] = r_bank
+
+        def turned_sums(n):
+            g, j = units[n]
+            r_bank = turned_banks.pop(n)
+            square_sums([r_bank[:, a, :] for a in range(GT)], [sums[g][:, a, 1 + j : 2 + j] for a in range(GT)])
+            if j == J - 1:
+                part_done(g)
+
+        relu_weight = INSTRUCTION + W // 2
+
+        def finish(g):
             box = {}
 
             def root():
-                o = stage.tile([P, CT * (J + 1)], F32, name="o", bufs=1)
-                nc.scalar.activation(out=o[:], in_=accs[c][:].rearrange("p a c -> p (a c)"), func=ACT.Sqrt)
-                box["o"] = o
+                roots = stage.tile([P, GT * (1 + J)], F32, name="roots", bufs=1)
+                nc.scalar.activation(out=roots[:], in_=sums[g][:].rearrange("p a c -> p (a c)"), func=ACT.Sqrt)
+                box["roots"] = roots
 
-            def neg():
-                o2 = stage.tile([P, CT, J + 1], F32, name="o2", bufs=2)
-                nc.vector.tensor_scalar(out=o2[:].rearrange("p a c -> p (a c)"), in0=box["o"][:], scalar1=-1.0, scalar2=None, op0=ALU.mult)
-                nc.sync.dma_start(out=ov[:, c * CT : (c + 1) * CT, :], in_=o2[:])
-
-            return [root, neg]
-
-        units = []
-        last = {}
-        for c in range(NCHUNK):
-            nd = CT - NA[c]
-            if nd:
-                jn = CT // nd
-                units += [(c, j, jn) for j in range(0, J, jn)]
-                last[c] = len(units) - 1
-        rt = {}
-        pst = {}
-
-        def relu(n):
-            c, j, jn = units[n]
-            nd = CT - NA[c]
-            r = work.tile([P, jn, nd * P], F32, name="r", bufs=8)
-            for k in range(jn):
+            def negate_and_store():
+                scores = stage.tile([P, GT, 1 + J], F32, name="scores")
                 nc.vector.tensor_scalar(
-                    out=r[:, k, :], in0=eTs[c][:, NA[c] * P : W], scalar1=nT[:, j + k : j + k + 1], scalar2=0.0, op0=ALU.subtract, op1=ALU.min
+                    out=scores[:].rearrange("p a c -> p (a c)"), in0=box["roots"][:], scalar1=-1.0, scalar2=None, op0=ALU.mult
                 )
-            rt[n] = r
+                nc.sync.dma_start(out=out_by_partition[:, g * GT : (g + 1) * GT, :], in_=scores[:])
 
-        def turn_r(n):
-            c, j, jn = units[n]
-            nd = CT - NA[c]
-            ps = psum.tile([P, jn, nd, D], F32, name="pss", tag="pss", bufs=PSS)
-            r = rt.pop(n)
-            for k in range(jn):
-                for a in range(nd):
-                    nc.tensor.transpose(ps[:, k, a, :], r[:, k, a * P : (a + 1) * P], ident[:])
-            pst[n] = ps
+            return [root] + wait * 4 + [negate_and_store]
 
-        def sumsq(n):
-            c, j, jn = units[n]
-            na = NA[c]
-            nd = CT - na
-            ps = pst.pop(n)
-            jk = work.tile([P, CT, D], BF16, name="jk", bufs=3)
-            for k in range(jn):
-                for a in range(nd):
-                    nc.scalar.activation(
-                        out=jk[:, k * nd + a, :], in_=ps[:, k, a, :], func=ACT.Square, accum_out=accs[c][:, na + a, 1 + j + k : 2 + j + k]
-                    )
+        n_units = len(units)
+        all_weight = (
+            sum(product_weight(k) for k in range(len(product_steps)))
+            + sum(relu_weight for n in range(n_units) if not on_scalar(n))
+            + len(direct_steps) * direct_weight
+            + NG * 28 * TASK
+        )
+        done_weight = 0
+        done_products = 0
+        done_direct = 0
+        sums_to_do = []
+        embedded = {0}
+        to_embed = list(range(1, NG))
+        task_list = []
+        embedding = None
 
-        steps_a = []
-        a_begin = {}
-        for c in range(NCHUNK):
-            if NA[c]:
-                a_begin[c] = len(steps_a)
-                ni = NA[c]
-                for s in range(J):
-                    steps_a.append((c, s, ni))
-        total = len(units)
-        n_a = len(steps_a)
-        done_a = 0
-        lag = 2
-        ready = set()
-        tasks = []
-        for c in range(NCHUNK):
-            tasks.append((START[c], c, "pro"))
-        queue = []
-        waiting = [c for c in range(NCHUNK) if c > 0]
-        fin = []
+        for task in embed(0):
+            task()
+        for n in range(RELU_AHEAD):
+            turned_relu(n)
+        for n in range(TURN_AHEAD):
+            turn_relu(n)
+        for n in range(n_units):
+            if n + RELU_AHEAD < n_units:
+                assert units[n + RELU_AHEAD][0] in embedded
+                turned_relu(n + RELU_AHEAD)
+                if not on_scalar(n + RELU_AHEAD):
+                    done_weight += relu_weight
+            if n + TURN_AHEAD < n_units:
+                turn_relu(n + TURN_AHEAD)
+            if unclipped:
+                direct_relu()
 
-        def a_step():
-            k = done_a
-            if k < n_a:
-                c, s, ni = steps_a[k]
-                max_j(c, s)
-                max_i(c, s * ni, ni)
-            if lag <= k < n_a + lag:
-                c, s, ni = steps_a[k - lag]
-                mul_n(c, s)
-                mul_e(c, s * ni, ni)
-                end = (s + 1) * ni
-                if end // (2 * P) > s * ni // (2 * P):
-                    fold_at.append((k + 1, c, s * ni // (2 * P)))
-                elif end == NA[c] * P:
-                    fold_at.append((k + 1, c, end // (2 * P)))
-                if s == J - 1:
-                    evac(c)
-                    fin.append((c, "a"))
-            while fold_at and fold_at[0][0] <= k:
-                q, c, pair = fold_at.pop(0)
-                fold(c, pair)
+            room = 4
+            while room > 0 and done_weight <= ((n + 1) * all_weight) // (n_units - TAIL):
+                product_ready = done_products <= len(product_steps) + PRODUCT_LAG and (
+                    done_products >= len(product_steps) or product_steps[done_products][0] in embedded
+                )
+                direct_ready = (
+                    done_direct < len(direct_steps)
+                    and direct_steps[done_direct][0] in embedded
+                    and len(sums_to_do) <= JD // 2 + 1
+                    and done_direct * (n_units - TAIL) <= n * len(direct_steps)
+                )
+                if direct_ready:
+                    direct_difference(*direct_steps[done_direct])
+                    sums_to_do += [(n + DIRECT_LAG + k // 2, *direct_steps[done_direct], k) for k in range(0, JD, 2)]
+                    done_weight += direct_weight
+                    room -= 3
+                    done_direct += 1
+                elif product_ready:
+                    product_step(done_products)
+                    done_weight += product_weight(done_products)
+                    room -= 2
+                    done_products += 1
+                else:
+                    break
 
-        fold_at = []
-        for s in prologue(0):
-            s()
-        ready.add(0)
-        done_d = set()
-        done_aa = set(c for c in range(NCHUNK) if NA[c] == 0)
-        current = -1
-        for n in range(-LA_R, total):
-            if n + LA_R < total:
-                assert units[n + LA_R][0] in ready
-                relu(n + LA_R)
-            if 0 <= n + LA_T < total:
-                turn_r(n + LA_T)
-            if n < 0:
-                continue
-            if not queue and waiting and n >= START[waiting[0]]:
-                current = waiting.pop(0)
-                queue = prologue(current)
-            elif not queue and fin:
-                c, kind = fin.pop(0)
-                if kind == "a":
-                    queue = combine(c)
-                    fin.insert(0, (c, "ac"))
-                elif kind == "ac":
-                    done_aa.add(c)
-                    if NA[c] == CT or c in done_d:
-                        queue = finish(c)
-                elif kind == "d":
-                    done_d.add(c)
-                    if c in done_aa:
-                        queue = finish(c)
-            if queue and n % SPACE == 0:
-                queue.pop(0)()
-                if not queue and current >= 0:
-                    ready.add(current)
-            goal = min(n_a + lag + 1, ((n - A_FIRST + 1) * (n_a + lag + 1)) // (total - A_FIRST - 16))
-            while done_a < goal:
-                if done_a < n_a:
-                    assert steps_a[done_a][0] in ready, (n, done_a)
-                a_step()
-                done_a += 1
-            sumsq(n)
-            c = units[n][0]
-            if last[c] == n:
-                fin.append((c, "d"))
-        while queue or fin:
-            if not queue:
-                c, kind = fin.pop(0)
-                if kind == "a":
-                    queue = combine(c)
-                    fin.insert(0, (c, "ac"))
-                elif kind == "ac":
-                    done_aa.add(c)
-                    if NA[c] == CT or c in done_d:
-                        queue = finish(c)
-                elif kind == "d":
-                    done_d.add(c)
-                    if c in done_aa:
-                        queue = finish(c)
-            else:
-                queue.pop(0)()
+            for k in range(3 if n < EARLY else 2 - n % 2):
+                if not task_list:
+                    embedding = None
+                    if ended:
+                        make, g = ended.pop(0)
+                        task_list = make(g)
+                    elif to_embed:
+                        embedding = to_embed.pop(0)
+                        task_list = embed(embedding)
+                if task_list:
+                    task = task_list.pop(0)
+                    task()
+                    if task is not pause:
+                        done_weight += TASK
+                    if not task_list and embedding is not None:
+                        embedded.add(embedding)
+
+            turned_sums(n)
+            for k in range(2):
+                if sums_to_do and sums_to_do[0][0] <= n:
+                    direct_sums(*sums_to_do.pop(0)[1:])
+
+        assert done_products == len(product_steps) + PRODUCT_LAG + 1 and done_direct == len(direct_steps) and not unclipped
+        while sums_to_do:
+            direct_sums(*sums_to_do.pop(0)[1:])
+        while task_list or ended:
+            if not task_list:
+                make, g = ended.pop(0)
+                task_list = make(g)
+            task_list.pop(0)()

from contextlib import ExitStack

import concourse.mybir as mybir
from concourse.masks import make_identity

B, K1, K2, D, J = 4096, 512, 512, 128, 128
P = 128
NT = B // P
GT = 4
W = GT * P
PACK = 4
FLOPS = 2 * B * (K1 * K2 + K2 * D) + 4 * B * (J + 1) * D

F32 = mybir.dt.float32
BF16 = mybir.dt.bfloat16
I32 = mybir.dt.int32
U32 = mybir.dt.uint32
U8 = mybir.dt.uint8
FP8 = mybir.dt.float8_e4m3fn
FP8X4 = mybir.dt.float8_e4m3fn_x4
FP4X4 = mybir.dt.float4_e2m1fn_x4
ALU = mybir.AluOpType
ACT = mybir.ActivationFunctionType
AX = mybir.AxisListType

WAYS = ["TTTT", "DDDD", "PPPP", "TTTT", "PPPP", "TTTT", "PPPP", "PPPD"]
NG = len(WAYS)

RELU_AHEAD = 5
TURN_AHEAD = 2
PRODUCT_LAG = 4
DIRECT_LAG = 3
PAUSE = 2

SCALAR_RELU = 4
JD = 8
EARLY = 30
TAIL = 12

INSTRUCTION = 24
TASK = 220


def tile_hypernymvisual_acc_t_w4_kernel(
    tc, vfs_bytes, vfs_scale, p_lfs, n_lfs, W_hidden_words, W_hidden_scales, b_hidden, W_embed_words, W_embed_scales, b_embed, out
):
    nc = tc.nc
    bytes_by_partition = vfs_bytes.rearrange("(p t) k -> p (t k)", t=NT)
    positives_by_partition = p_lfs.rearrange("(p t) d -> p t d", t=NT)
    out_by_partition = out.rearrange("(p t) c -> p t c", t=NT)

    with ExitStack() as ctx:
        keep = ctx.enter_context(tc.tile_pool(name="keep", bufs=1))
        stage = ctx.enter_context(tc.tile_pool(name="stage", bufs=2))
        work = ctx.enter_context(tc.tile_pool(name="work", bufs=2))
        psum = ctx.enter_context(tc.psum_pool(name="psum", bufs=1))
        ctx.enter_context(tc.manual_schedule())

        code_bytes = {}

        def load_bytes(g):
            x_bytes = stage.tile([P, GT * K1], U8, name="x_bytes", bufs=4)
            nc.sync.dma_start(out=x_bytes[:], in_=bytes_by_partition[:, g * GT * K1 : (g + 1) * GT * K1])
            code_bytes[g] = x_bytes

        load_bytes(0)
        x_scale = keep.tile([P, K1], F32, name="x_scale")
        nc.sync.dma_start(out=x_scale[:], in_=vfs_scale.rearrange("o k -> (o k)").partition_broadcast(P))
        wh_raw = keep.tile([P, 2 * K2], U8, name="wh_raw")
        nc.sync.dma_start(out=wh_raw[:].bitcast(I32), in_=W_hidden_words[0].bitcast(I32))
        we = keep.tile([P, 2 * D], U8, name="we", align_bytes=64)
        nc.sync.dma_start(out=we[:].bitcast(I32), in_=W_embed_words[0].bitcast(I32))
        wh_scales_raw = keep.tile([P, K2], U8, name="wh_scales_raw")
        we_scales = keep.tile([P, D], U8, name="we_scales", align_bytes=64)
        nc.vector.memset(wh_scales_raw[:].bitcast(I32), 0)
        nc.vector.memset(we_scales[:].bitcast(I32), 0)
        for q in range(4):
            nc.sync.dma_start(
                out=wh_scales_raw[32 * q : 32 * q + 4, :].bitcast(I32), in_=W_hidden_scales[0, 4 * q : 4 * q + 4, :].bitcast(I32)
            )
        for q in range(4):
            nc.sync.dma_start(
                out=we_scales[32 * q : 32 * q + 4, :].bitcast(I32), in_=W_embed_scales[0, 4 * q : 4 * q + 4, :].bitcast(I32)
            )
        bias_hidden = keep.tile([P, PACK], BF16, name="bias_hidden")
        nc.sync.dma_start(out=bias_hidden[:], in_=b_hidden.rearrange("(p t) -> p t", t=PACK))
        bias_embed = keep.tile([P, 1], BF16, name="bias_embed")
        nc.sync.dma_start(out=bias_embed[:], in_=b_embed.rearrange("(d o) -> d o", o=1))
        n_rows = keep.tile([P, D], BF16, name="n_rows")
        nc.sync.dma_start(out=n_rows[:], in_=n_lfs)
        load_bytes(1)
        positives = keep.tile([P, NT, D], BF16, name="positives")
        nc.sync.dma_start(out=positives[:], in_=positives_by_partition)
        load_bytes(2)
        load_bytes(3)
        n_spread = keep.tile([P, J * D], BF16, name="n_spread")
        nc.sync.dma_start(out=n_spread[:], in_=n_lfs.rearrange("j d -> (j d)").partition_broadcast(P))

        one = keep.tile([P, 1], F32, name="one")
        nc.vector.memset(one[:], 1.0)
        first_root = keep.tile([P, 1], F32, name="first_root")
        nc.scalar.activation(out=first_root[:], in_=one[:], func=ACT.Sqrt)
        ident = keep.tile([P, P], F32, name="ident")
        make_identity(nc, ident[:])

        wh = keep.tile([P, 2 * K2], U8, name="wh", align_bytes=64)
        wh_scales = keep.tile([P, K2], U8, name="wh_scales", align_bytes=64)
        n32 = keep.tile([P, D], F32, name="n32")
        nT = keep.tile([P, J], F32, name="nT")
        nT_bf = keep.tile([P, J], BF16, name="nT_bf")
        nT_minus = keep.tile([P, J], BF16, name="nT_minus")

        def arrange_weights():
            nc.vector.tensor_copy(
                out=wh[:].rearrange("p (t m b) -> p t m b", t=PACK, b=2), in_=wh_raw[:].rearrange("p (m t b) -> p t m b", t=PACK, b=2)
            )
            nc.vector.tensor_copy(
                out=wh_scales[:].rearrange("p (t m) -> p t m", t=PACK), in_=wh_scales_raw[:].rearrange("p (m t) -> p t m", t=PACK)
            )

        def arrange_negatives():
            nc.vector.tensor_copy(out=n32[:], in_=n_rows[:])
            turned_n = psum.tile([P, J], F32, name="turned_n", tag="task", bufs=1)
            nc.tensor.transpose(turned_n[:], n32[:], ident[:])
            nc.vector.tensor_copy(out=nT[:], in_=turned_n[:])
            nc.vector.tensor_copy(out=nT_bf[:], in_=nT[:])
            nc.vector.tensor_scalar(out=nT_minus[:], in0=nT[:], scalar1=-1.0, scalar2=None, op0=ALU.mult)

        eT = {}
        e_rows = {}
        e_high = {}
        e_parts = {}
        e_squares = {}
        sums = {}
        parts_done = {}
        ended = []

        def part_done(g):
            parts_done[g] = parts_done.get(g, 0) + 1
            if parts_done[g] == len(set(WAYS[g])):
                ended.append((finish, g))

        def pause():
            pass

        wait = [pause] * PAUSE

        def square_sums(sources, targets):
            squares = work.tile([P, len(sources), D], BF16, name="squares", bufs=3)
            for k in range(len(sources)):
                nc.scalar.activation(out=squares[:, k, :], in_=sources[k], func=ACT.Square, accum_out=targets[k])

        def embed(g):
            n_p = WAYS[g].count("P")
            n_d = WAYS[g].count("D")
            box = {}
            rows = []
            eT_g = stage.tile([P, W], F32, name="eT_g", bufs=6)
            sums_g = stage.tile([P, GT, 1 + J], F32, name="sums_g", bufs=NG)
            eT[g] = eT_g
            sums[g] = sums_g

            def bank(name, shape):
                if g == 0:
                    return psum.tile(shape, F32, name=name, tag="turned", bufs=4)
                return psum.tile(shape, F32, name=name, tag="task", bufs=1)

            def widen(a):
                x = stage.tile([P, K1], BF16, name="x", bufs=4)
                nc.vector.tensor_tensor(
                    out=x[:], in0=code_bytes[g][:, a * K1 : (a + 1) * K1].bitcast(FP8), in1=x_scale[:], op=ALU.mult
                )
                rows.append(x)

            def turn_x(b):
                xT = bank("xT", [P, 2, 2, P])
                for a in range(2):
                    words = rows[2 * b + a][:].bitcast(F32)
                    for u in range(2):
                        nc.tensor.transpose(xT[:, a, u, :], words[:, u : K1 // 2 : 2], ident[:])
                box["xT"] = xT

            def unload_x(b):
                if b == 0:
                    x_packed = stage.tile([P, PACK * W], BF16, name="x_packed", align_bytes=64)
                    box["x_packed"] = x_packed
                half = box["x_packed"][:].bitcast(F32)[:, b * W : (b + 1) * W]
                nc.scalar.copy(
                    out=half.rearrange("p (a r u) -> p a r u", a=2, u=2), in_=box["xT"][:].rearrange("p a u r -> p a r u")
                )

            def quantise_x():
                x_codes = stage.tile([P, W], U32, name="x_codes", align_bytes=64)
                x_scales = stage.tile([P, W], U8, name="x_scales", align_bytes=64)
                nc.vector.quantize_mx(out=x_codes[:].bitcast(FP8X4), scales=x_scales[:], in_=box["x_packed"][:])
                box["x_codes"] = x_codes
                box["x_scales"] = x_scales

            def multiply_x(a):
                hT = bank("hT", [P, PACK, P])
                cols = slice(a * P, (a + 1) * P)
                for t in range(PACK):
                    nc.tensor.matmul_mx(
                        out=hT[:, t, :],
                        lhsT=wh[:, 2 * P * t : 2 * P * (t + 1)].bitcast(FP4X4),
                        lhsT_scale=wh_scales[:, P * t : P * (t + 1)],
                        rhs=box["x_codes"][:, cols].bitcast(FP8X4),
                        rhs_scale=box["x_scales"][:, cols],
                        start=True,
                        stop=True,
                    )
                box["hT"] = hT

            def add_bias(a):
                if a == 0:
                    h_packed = stage.tile([P, PACK * W], BF16, name="h_packed", align_bytes=64)
                    box["h_packed"] = h_packed
                nc.vector.tensor_tensor(
                    out=box["h_packed"][:, PACK * P * a : PACK * P * (a + 1)].rearrange("p (r t) -> p r t", t=PACK),
                    in0=box["hT"][:].rearrange("p t r -> p r t"),
                    in1=bias_hidden[:].unsqueeze(1).to_broadcast([P, P, PACK]),
                    op=ALU.add,
                )

            def quantise_h():
                h_codes = stage.tile([P, W], U32, name="h_codes", align_bytes=64)
                h_scales = stage.tile([P, W], U8, name="h_scales", align_bytes=64)
                nc.vector.quantize_mx(out=h_codes[:].bitcast(FP8X4), scales=h_scales[:], in_=box["h_packed"][:])
                box["h_codes"] = h_codes
                box["h_scales"] = h_scales

            def multiply_h():
                raw_eT = bank("raw_eT", [P, W])
                nc.tensor.matmul_mx(
                    out=raw_eT[:],
                    lhsT=we[:].bitcast(FP4X4),
                    lhsT_scale=we_scales[:],
                    rhs=box["h_codes"][:].bitcast(FP8X4),
                    rhs_scale=box["h_scales"][:],
                    start=True,
                    stop=True,
                )
                box["raw_eT"] = raw_eT

            def unload_e():
                nc.scalar.activation(out=eT_g[:], in_=box["raw_eT"][:], func=ACT.Identity, bias=bias_embed[:, 0:1])

            def turn_e():
                e_bank = bank("e_bank", [P, GT, D])
                for a in range(GT):
                    nc.tensor.transpose(e_bank[:, a, :], eT_g[:, a * P : (a + 1) * P], ident[:])
                box["e_bank"] = e_bank

            def positive_difference():
                x_pos = stage.tile([P, GT, D], F32, name="x_pos", bufs=1)
                nc.vector.tensor_tensor(
                    out=x_pos[:], in0=box["e_bank"][:], in1=positives[:, g * GT : (g + 1) * GT, :], op=ALU.subtract
                )
                box["x_pos"] = x_pos

            def keep_e_rows():
                if n_p:
                    e_squares_g = stage.tile([P, n_p], F32, name="e_squares_g", bufs=3)
                    square_sums([box["e_bank"][:, a, :] for a in range(n_p)], [e_squares_g[:, a : a + 1] for a in range(n_p)])
                    e_squares[g] = e_squares_g
                if n_d:
                    e_rows_g = stage.tile([P, n_d, D], F32, name="e_rows_g", bufs=2)
                    nc.scalar.copy(out=e_rows_g[:], in_=box["e_bank"][:, GT - n_d : GT, :])
                    e_rows[g] = e_rows_g

            def positive_relu():
                r_pos = stage.tile([P, GT, D], F32, name="r_pos", bufs=1)
                nc.vector.tensor_scalar(out=r_pos[:], in0=box["x_pos"][:], scalar1=0.0, scalar2=None, op0=ALU.min)
                box["r_pos"] = r_pos

            def positive_sums():
                square_sums([box["r_pos"][:, a, :] for a in range(GT)], [sums_g[:, a, 0:1] for a in range(GT)])

            def split_e():
                e_high_g = stage.tile([P, n_p * P], BF16, name="e_high_g", bufs=3)
                e_parts_g = stage.tile([P, 2, n_p * P], BF16, name="e_parts_g", bufs=3)
                e_p = eT_g[:, 0 : n_p * P]
                nc.vector.tensor_copy(out=e_high_g[:], in_=e_p)
                nc.vector.tensor_scalar(out=e_parts_g[:, 0, :], in0=e_high_g[:], scalar1=0.5, scalar2=None, op0=ALU.mult)
                nc.vector.scalar_tensor_tensor(
                    out=e_parts_g[:, 1, :], in0=e_high_g[:], scalar=-1.0, in1=e_p, op0=ALU.mult, op1=ALU.add
                )
                e_high[g] = e_high_g
                e_parts[g] = e_parts_g

            tasks = [lambda a=a: widen(a) for a in range(GT)]
            for b in range(2):
                tasks += [lambda b=b: turn_x(b)] + wait + [lambda b=b: unload_x(b)]
            if g + 4 < NG:
                tasks.append(lambda: load_bytes(g + 4))
            if g == 0:
                tasks += [arrange_weights, arrange_negatives]
            tasks += wait + [quantise_x] + wait
            for a in range(GT):
                tasks += [lambda a=a: multiply_x(a)] + wait + [lambda a=a: add_bias(a)]
            tasks += [quantise_h] + wait + [multiply_h] + wait + [unload_e] + wait
            tasks += [turn_e] + wait + [positive_difference, keep_e_rows, positive_relu] + wait + [positive_sums]
            if n_p:
                tasks.append(split_e)
            return tasks

        m_rows = {}
        m_negatives = {}
        m_n = {}
        m_e = {}
        m_e_sums = {}
        m_n_sums = {}

        def make_m_rows(g, j):
            m_row = work.tile([P, WAYS[g].count("P") * P], BF16, name="m_row", bufs=PRODUCT_LAG + 3)
            nc.vector.tensor_scalar(out=m_row[:], in0=e_high[g][:], scalar1=nT[:, j : j + 1], scalar2=None, op0=ALU.max)
            m_rows[g, j] = m_row

        def multiply_n(g, j):
            n_p = WAYS[g].count("P")
            if j == 0:
                m_n_bank = psum.tile([P, n_p, J], F32, name="m_n_bank", tag="m_n", bufs=1)
                m_n[g] = m_n_bank
            m_row = m_rows.pop((g, j))
            for a in range(n_p):
                nc.tensor.matmul(
                    m_n[g][:, a, j : j + 1], lhsT=m_row[:, a * P : (a + 1) * P], rhs=nT_bf[:, j : j + 1], start=True, stop=True
                )

        def make_m_negatives(g, i0, ni):
            m_negative = work.tile([P, ni, J], BF16, name="m_negative", bufs=PRODUCT_LAG + 3)
            for k in range(ni):
                nc.vector.tensor_scalar(
                    out=m_negative[:, k, :], in0=nT_bf[:], scalar1=e_high[g][:, i0 + k : i0 + k + 1], scalar2=None, op0=ALU.max
                )
            m_negatives[g, i0] = m_negative

        def multiply_e(g, i0, ni):
            m_negative = m_negatives.pop((g, i0))
            for k in range(ni):
                half, col = divmod(i0 + k, 2 * P)
                if col == 0:
                    m_e_bank = psum.tile([P, 2 * P, 2], F32, name="m_e_bank", tag="m_e", bufs=2)
                    m_e[g, half] = m_e_bank
                nc.tensor.matmul(
                    m_e[g, half][:, col, :], lhsT=m_negative[:, k, :], rhs=e_parts[g][:, :, i0 + k], start=True, stop=True
                )

        def fold(g, half):
            n_rows_p = WAYS[g].count("P") * P
            begin, end = 2 * P * half, min(2 * P * (half + 1), n_rows_p)
            if half == 0:
                m_e_sum = stage.tile([P, n_rows_p], F32, name="m_e_sum")
                m_e_sums[g] = m_e_sum
            nc.vector.tensor_reduce(out=m_e_sums[g][:, begin:end], in_=m_e[g, half][:, 0 : end - begin, :], axis=AX.X, op=ALU.add)

        def unload_m_n(g):
            n_p = WAYS[g].count("P")
            m_n_sum = stage.tile([P, n_p, J], F32, name="m_n_sum")
            for a in range(n_p):
                nc.scalar.activation(out=m_n_sum[:, a, :], in_=m_n[g][:, a, :], func=ACT.Identity, bias=e_squares[g][:, a : a + 1])
            m_n_sums[g] = m_n_sum

        def combine(g):
            n_p = WAYS[g].count("P")
            box = {}

            def multiply_n_eh():
                n_eh = psum.tile([P, n_p, J], F32, name="n_eh", tag="task", bufs=1)
                for a in range(n_p):
                    nc.tensor.matmul(n_eh[:, a, :], lhsT=e_high[g][:, a * P : (a + 1) * P], rhs=nT_minus[:], start=True, stop=True)
                box["n_eh"] = n_eh

            def add_n_eh():
                without_m_e = stage.tile([P, n_p, J], F32, name="without_m_e", bufs=1)
                nc.vector.tensor_tensor(out=without_m_e[:], in0=box["n_eh"][:], in1=m_n_sums[g][:], op=ALU.add)
                box["without_m_e"] = without_m_e

            def turn_m_e():
                m_e_turned = psum.tile([P, n_p, J], F32, name="m_e_turned", tag="task", bufs=1)
                for a in range(n_p):
                    nc.tensor.transpose(m_e_turned[:, a, :], m_e_sums[g][:, a * P : (a + 1) * P], ident[:])
                box["m_e_turned"] = m_e_turned

            def add_m_e():
                total = stage.tile([P, n_p, J], F32, name="total", bufs=1)
                nc.vector.scalar_tensor_tensor(
                    out=total[:], in0=box["m_e_turned"][:], scalar=-2.0, in1=box["without_m_e"][:], op0=ALU.mult, op1=ALU.add
                )
                box["total"] = total

            def clip():
                nc.vector.tensor_scalar(out=sums[g][:, 0:n_p, 1 : 1 + J], in0=box["total"][:], scalar1=0.0, scalar2=None, op0=ALU.max)
                part_done(g)

            return [multiply_n_eh] + wait + [add_n_eh, turn_m_e] + wait + [add_m_e, clip]

        product_steps = [(g, s, WAYS[g].count("P")) for g in range(NG) if "P" in WAYS[g] for s in range(J)]
        folds = []

        def product_step(k):
            if k < len(product_steps):
                g, s, ni = product_steps[k]
                make_m_rows(g, s)
                make_m_negatives(g, s * ni, ni)
            if PRODUCT_LAG <= k < len(product_steps) + PRODUCT_LAG:
                g, s, ni = product_steps[k - PRODUCT_LAG]
                multiply_n(g, s)
                multiply_e(g, s * ni, ni)
                half, end = s * ni // (2 * P), (s + 1) * ni
                last = end == ni * P
                if end // (2 * P) > half or last:
                    folds.append((k + 1, g, half, last))
                if s == J - 1:
                    unload_m_n(g)
            while folds and folds[0][0] <= k:
                after, g, half, last = folds.pop(0)
                fold(g, half)
                if last:
                    ended.append((combine, g))

        def product_weight(k):
            g, s, ni = product_steps[min(k, len(product_steps) - 1)]
            return INSTRUCTION * (1 + ni) + ni * P // 4 + ni * J // 4

        direct_steps = [(g, a, q) for g in range(NG) for a in range(WAYS[g].count("D")) for q in range(J // JD)]
        direct_relus = {}
        unclipped = []

        def direct_difference(g, a, q):
            x_dir = work.tile([P, JD, D], F32, name="x_dir")
            r_dir = work.tile([P, JD * D], F32, name="r_dir", bufs=4)
            nc.vector.tensor_tensor(
                out=x_dir[:],
                in0=n_spread[:, q * JD * D : (q + 1) * JD * D].rearrange("p (j d) -> p j d", d=D),
                in1=e_rows[g][:, a : a + 1, :].to_broadcast([P, JD, D]),
                op=ALU.subtract,
            )
            direct_relus[g, a, q] = r_dir
            unclipped.append((x_dir, r_dir))

        def direct_relu():
            x_dir, r_dir = unclipped.pop(0)
            nc.vector.tensor_scalar(out=r_dir[:], in0=x_dir[:].rearrange("p j d -> p (j d)"), scalar1=0.0, scalar2=None, op0=ALU.max)

        def direct_sums(g, a, q, k0):
            tile = GT - WAYS[g].count("D") + a
            ks = range(k0, k0 + 2)
            square_sums(
                [direct_relus[g, a, q][:, k * D : (k + 1) * D] for k in ks],
                [sums[g][:, tile, 1 + q * JD + k : 2 + q * JD + k] for k in ks],
            )
            if (a + 1, q + 1, k0 + 2) == (WAYS[g].count("D"), J // JD, JD):
                part_done(g)

        direct_weight = 2 * INSTRUCTION + JD * D + JD * D // 2

        units = [(g, j) for g in range(NG) if WAYS[g] == "TTTT" for j in range(J)]
        turned_relus = {}
        turned_banks = {}

        def on_scalar(n):
            return n % SCALAR_RELU == SCALAR_RELU - 1

        def turned_relu(n):
            g, j = units[n]
            r = work.tile([P, W], F32, name="r", bufs=8)
            if on_scalar(n):
                nc.scalar.activation(out=r[:], in_=eT[g][:], func=ACT.Relu, scale=-1.0, bias=nT[:, j : j + 1])
            else:
                nc.vector.tensor_scalar(out=r[:], in0=eT[g][:], scalar1=nT[:, j : j + 1], scalar2=0.0, op0=ALU.subtract, op1=ALU.min)
            turned_relus[n] = r

        def turn_relu(n):
            r_bank = psum.tile([P, GT, D], F32, name="r_bank", tag="turned", bufs=4)
            r = turned_relus.pop(n)
            for a in range(GT):
                nc.tensor.transpose(r_bank[:, a, :], r[:, a * P : (a + 1) * P], ident[:])
            turned_banks[n] = r_bank

        def turned_sums(n):
            g, j = units[n]
            r_bank = turned_banks.pop(n)
            square_sums([r_bank[:, a, :] for a in range(GT)], [sums[g][:, a, 1 + j : 2 + j] for a in range(GT)])
            if j == J - 1:
                part_done(g)

        relu_weight = INSTRUCTION + W // 2

        def finish(g):
            box = {}

            def root():
                roots = stage.tile([P, GT * (1 + J)], F32, name="roots", bufs=1)
                nc.scalar.activation(out=roots[:], in_=sums[g][:].rearrange("p a c -> p (a c)"), func=ACT.Sqrt)
                box["roots"] = roots

            def negate_and_store():
                scores = stage.tile([P, GT, 1 + J], F32, name="scores")
                nc.vector.tensor_scalar(
                    out=scores[:].rearrange("p a c -> p (a c)"), in0=box["roots"][:], scalar1=-1.0, scalar2=None, op0=ALU.mult
                )
                nc.sync.dma_start(out=out_by_partition[:, g * GT : (g + 1) * GT, :], in_=scores[:])

            return [root] + wait * 4 + [negate_and_store]

        n_units = len(units)
        all_weight = (
            sum(product_weight(k) for k in range(len(product_steps)))
            + sum(relu_weight for n in range(n_units) if not on_scalar(n))
            + len(direct_steps) * direct_weight
            + NG * 28 * TASK
        )
        done_weight = 0
        done_products = 0
        done_direct = 0
        sums_to_do = []
        embedded = {0}
        to_embed = list(range(1, NG))
        task_list = []
        embedding = None

        for task in embed(0):
            task()
        for n in range(RELU_AHEAD):
            turned_relu(n)
        for n in range(TURN_AHEAD):
            turn_relu(n)
        for n in range(n_units):
            if n + RELU_AHEAD < n_units:
                assert units[n + RELU_AHEAD][0] in embedded
                turned_relu(n + RELU_AHEAD)
                if not on_scalar(n + RELU_AHEAD):
                    done_weight += relu_weight
            if n + TURN_AHEAD < n_units:
                turn_relu(n + TURN_AHEAD)
            if unclipped:
                direct_relu()

            room = 4
            while room > 0 and done_weight <= ((n + 1) * all_weight) // (n_units - TAIL):
                product_ready = done_products <= len(product_steps) + PRODUCT_LAG and (
                    done_products >= len(product_steps) or product_steps[done_products][0] in embedded
                )
                direct_ready = (
                    done_direct < len(direct_steps)
                    and direct_steps[done_direct][0] in embedded
                    and len(sums_to_do) <= JD // 2 + 1
                    and done_direct * (n_units - TAIL) <= n * len(direct_steps)
                )
                if direct_ready:
                    direct_difference(*direct_steps[done_direct])
                    sums_to_do += [(n + DIRECT_LAG + k // 2, *direct_steps[done_direct], k) for k in range(0, JD, 2)]
                    done_weight += direct_weight
                    room -= 3
                    done_direct += 1
                elif product_ready:
                    product_step(done_products)
                    done_weight += product_weight(done_products)
                    room -= 2
                    done_products += 1
                else:
                    break

            for k in range(3 if n < EARLY else 2 - n % 2):
                if not task_list:
                    embedding = None
                    if ended:
                        make, g = ended.pop(0)
                        task_list = make(g)
                    elif to_embed:
                        embedding = to_embed.pop(0)
                        task_list = embed(embedding)
                if task_list:
                    task = task_list.pop(0)
                    task()
                    if task is not pause:
                        done_weight += TASK
                    if not task_list and embedding is not None:
                        embedded.add(embedding)

            turned_sums(n)
            for k in range(2):
                if sums_to_do and sums_to_do[0][0] <= n:
                    direct_sums(*sums_to_do.pop(0)[1:])

        assert done_products == len(product_steps) + PRODUCT_LAG + 1 and done_direct == len(direct_steps) and not unclipped
        while sums_to_do:
            direct_sums(*sums_to_do.pop(0)[1:])
        while task_list or ended:
            if not task_list:
                make, g = ended.pop(0)
                task_list = make(g)
            task_list.pop(0)()
